import numpy as np
import ml_dtypes


def mxq(x, axis, fmt="e4m3"):
    dtype, down = {"e4m3": (ml_dtypes.float8_e4m3fn, 7), "e5m2": (ml_dtypes.float8_e5m2, 14)}[fmt]
    v = np.moveaxis(np.asarray(x, np.float32).astype(ml_dtypes.bfloat16).astype(np.float64), axis, -1)
    blocks = v.reshape(v.shape[:-1] + (-1, 32))
    amax = np.abs(blocks).max(-1, keepdims=True)
    byte = np.maximum(np.where(amax > 0, np.frexp(amax)[1] - 1 + 127, 0) - down, 1)
    scale = np.exp2(byte - 127.0)
    codes = (blocks / scale).astype(np.float32).astype(dtype).astype(np.float64)
    return np.moveaxis((codes * scale).reshape(v.shape), -1, axis)


WIDE = False


def mx_kscale(k):
    if not WIDE:
        return np.ones(k)
    levels = np.array([10, -10, 5, -5, 0])
    a = np.random.permutation(np.resize(levels, k // 512 * 4)).reshape(k // 512, 4)
    idx = np.arange(k)
    return np.exp2(a[idx // 512, idx % 128 // 32])


BF16 = ml_dtypes.bfloat16


def bf(x):
    return np.asarray(x, np.float32).astype(BF16)


def f64(x):
    return np.asarray(x).astype(np.float64)


E2M1 = np.array([0.0, 0.5, 1.0, 1.5, 2.0, 3.0, 4.0, 6.0, -0.0, -0.5, -1.0, -1.5, -2.0, -3.0, -4.0, -6.0])


def pack_weight(w, fmt):
    k, n = w.shape
    w = f64(bf(w)).reshape(k // 32, 32, n)
    amax = np.abs(w).max(1)
    if fmt == "e4m3":
        byte = np.frexp(amax)[1] - 1 + 127 - 7
    else:
        mant, ex = np.frexp(amax / 6.0)
        byte = np.where(mant > 0.5, ex, ex - 1) + 127
    byte = np.clip(np.where(amax > 0, byte, 1), 1, 254)
    scaled = (w * np.exp2(127.0 - byte)[:, None, :]).reshape(k, n).astype(np.float32)
    by_word = np.ascontiguousarray(scaled.reshape(k // 512, 128, 4, n).transpose(0, 1, 3, 2))
    if fmt == "e4m3":
        words = by_word.astype(ml_dtypes.float8_e4m3fn).view(np.uint8)
    else:
        c = by_word.astype(ml_dtypes.float4_e2m1fn).view(np.uint8) & 0xF
        words = c[..., 0::2] | (c[..., 1::2] << 4)
    return np.ascontiguousarray(words), np.ascontiguousarray(byte.astype(np.uint8).reshape(k // 512, 16, n))


def unpack_weight(words, scales, fmt):
    g, p, n, _ = words.shape
    if fmt == "e4m3":
        vals = np.ascontiguousarray(words).view(ml_dtypes.float8_e4m3fn).astype(np.float64)
    else:
        nib = np.empty((g, p, n, 4), np.uint8)
        nib[..., 0::2] = words & 0xF
        nib[..., 1::2] = words >> 4
        vals = E2M1[nib]
    vals = vals * np.repeat(np.exp2(scales.astype(np.float64) - 127.0), 8, axis=1)[..., None]
    return vals.transpose(0, 1, 3, 2).reshape(g * 512, n)


B, N, E, L, A, H1, H2, G = 256, 8, 8, 384, 128, 1024, 1024, 8


def mish(v):
    return v * np.tanh(np.log(1.0 + np.exp(v)))


def simnorm(v):
    vg = v.reshape(v.shape[:-1] + (v.shape[-1] // G, G))
    ex = np.exp(vg - vg.max(-1, keepdims=True))
    return (ex / ex.sum(-1, keepdims=True)).reshape(v.shape)


def setup_inputs():
    s = mx_kscale(H2)
    r = np.random.standard_normal
    h2 = bf(mish(r((B, E, H2))) * s)
    logits = bf(r((B, N, E)))
    stack = r((E, H2, L)) * 2.0 / np.sqrt(H2) / s[:, None]
    words, scales = pack_weight(stack.reshape(-1, L), "e4m3")
    b3 = bf(0.3 * r((E, L)))
    return {"h2": h2,
            "logits": logits,
            "W3_words": words,
            "W3_scales": scales,
            "b3": b3}


def reference(h2, logits, W3_words, W3_scales, b3):
    hq = mxq(f64(h2).transpose(1, 0, 2), 2, "e4m3")
    z = (hq @ unpack_weight(W3_words, W3_scales, "e4m3").reshape(E, H2, L)) + f64(b3)[:, None, :]
    y = simnorm(z)
    lg = f64(logits)
    ex = np.exp(lg - lg.max(-1, keepdims=True))
    comb = ex / ex.sum(-1, keepdims=True)
    return sum(comb[:, :, e, None] * y[e][:, None, :] for e in range(E))

@@ -1,0 +1,309 @@
+from contextlib import ExitStack
+
+import concourse.mybir as mybir
+from concourse.masks import make_identity
+
+F32 = mybir.dt.float32
+BF16 = mybir.dt.bfloat16
+I32 = mybir.dt.int32
+U32 = mybir.dt.uint32
+U8 = mybir.dt.uint8
+FP8X4 = mybir.dt.float8_e4m3fn_x4
+ALU = mybir.AluOpType
+ACT = mybir.ActivationFunctionType
+AXIS = mybir.AxisListType
+
+P = 128
+PACK = 4
+K_PASS = P * PACK
+
+BATCH = 256
+EXPERTS = 8
+AGENTS = 8
+FEATURES = 1024
+COLS = 384
+GROUP = 8
+
+PASSES = FEATURES // K_PASS
+ROW_TILES = BATCH // P
+CHUNKS = COLS // P
+BANK = 512
+
+TENSOR_CHUNKS = 2
+TENSOR_COLS = TENSOR_CHUNKS * P
+ROWS_PER_BLOCK = P // EXPERTS
+BLOCKS = BATCH // ROWS_PER_BLOCK
+
+FLOPS = 2 * BATCH * EXPERTS * FEATURES * COLS + 2 * BATCH * AGENTS * EXPERTS * COLS
+
+
+def group_softmax(nc, work, z, y, width):
+    groups = width // GROUP
+    shape = [P, groups, GROUP]
+    z_groups = z.rearrange("p (g i) -> p g i", i=GROUP)
+    top = work.tile([P, groups], F32)
+    nc.vector.tensor_reduce(out=top[:], in_=z_groups, axis=AXIS.X, op=ALU.max)
+    powers = work.tile(shape, F32)
+    nc.vector.tensor_tensor(
+        out=powers[:], in0=z_groups, in1=top[:].unsqueeze(2).to_broadcast(shape), op=ALU.subtract
+    )
+    nc.scalar.activation(out=powers[:], in_=powers[:], func=ACT.Exp)
+    total = work.tile([P, groups], F32)
+    nc.vector.tensor_reduce(out=total[:], in_=powers[:], axis=AXIS.X, op=ALU.add)
+    inverse = work.tile([P, groups], F32)
+    nc.vector.reciprocal(out=inverse[:], in_=total[:])
+    nc.gpsimd.tensor_tensor(
+        out=y.rearrange("p (g i) -> p g i", i=GROUP),
+        in0=powers[:],
+        in1=inverse[:].unsqueeze(2).to_broadcast(shape),
+        op=ALU.mult,
+    )
+
+
+def tile_softmoedynamics_pb_e_kernel(tc, h2, logits, W3_words, W3_scales, b3, out):
+    nc = tc.nc
+    with ExitStack() as ctx:
+        keep = ctx.enter_context(tc.tile_pool(name="keep", bufs=1))
+        work = ctx.enter_context(tc.tile_pool(name="work", bufs=3))
+        psum = ctx.enter_context(tc.psum_pool(name="psum", bufs=2))
+
+        h2_rows = keep.tile([P, ROW_TILES, EXPERTS, FEATURES], BF16)
+        w_words = keep.tile([P, EXPERTS * PASSES, COLS], U32, align_bytes=64)
+        w_scales = keep.tile([P, EXPERTS * PASSES, COLS], U8, align_bytes=64)
+        nc.vector.memset(w_scales[:].bitcast(I32), 0)
+
+        def load_expert(e):
+            passes = slice(e * PASSES, (e + 1) * PASSES)
+            nc.sync.dma_start(
+                out=h2_rows[:, :, e, :], in_=h2[:, e, :].rearrange("(t b) k -> b t k", b=P)
+            )
+            nc.sync.dma_start(
+                out=w_words[:, passes, :].bitcast(I32),
+                in_=W3_words[passes].rearrange("g p n t -> p g (n t)").bitcast(I32),
+            )
+
+        load_expert(0)
+        for quadrant in range(4):
+            nc.sync.dma_start(
+                out=w_scales[32 * quadrant : 32 * quadrant + 4, :, :].bitcast(I32),
+                in_=W3_scales[:, 4 * quadrant : 4 * quadrant + 4, :]
+                .rearrange("g r n -> r g n")
+                .bitcast(I32),
+            )
+        for e in range(1, EXPERTS):
+            load_expert(e)
+
+        identity = keep.tile([P, P], F32)
+        make_identity(nc, identity[:])
+
+        b3_rows = keep.tile([P, COLS], BF16)
+        nc.vector.memset(b3_rows[:], 0.0)
+        nc.scalar.dma_start(out=b3_rows[0:EXPERTS, :], in_=b3[:, :])
+        b3_wide = keep.tile([P, COLS], F32)
+        nc.vector.tensor_copy(out=b3_wide[:], in_=b3_rows[:])
+        b3_ps = psum.tile([P, CHUNKS, P], F32, tag="sum")
+        for c in range(CHUNKS):
+            nc.tensor.transpose(b3_ps[:, c, :], b3_wide[:, c * P : (c + 1) * P], identity[:])
+        bias = keep.tile([P, CHUNKS, EXPERTS], F32)
+        nc.vector.tensor_copy(out=bias[:], in_=b3_ps[:, :, 0:EXPERTS])
+
+        logit_rows = keep.tile([P, ROW_TILES, AGENTS * EXPERTS], BF16)
+        nc.scalar.dma_start(
+            out=logit_rows[:], in_=logits.rearrange("(t b) n e -> b t (n e)", b=P)
+        )
+        mix_rows = keep.tile([P, ROW_TILES, AGENTS, EXPERTS], F32)
+        group_softmax(
+            nc,
+            work,
+            logit_rows[:].rearrange("b t c -> b (t c)"),
+            mix_rows[:].rearrange("b t n e -> b (t n e)"),
+            ROW_TILES * AGENTS * EXPERTS,
+        )
+
+        logit_blocks = keep.tile([P, ROWS_PER_BLOCK, EXPERTS], BF16)
+        for n in range(AGENTS):
+            nc.gpsimd.dma_start(
+                out=logit_blocks[n * BLOCKS : (n + 1) * BLOCKS, :, :],
+                in_=logits[:, n, :].rearrange("(j i) e -> j i e", i=ROWS_PER_BLOCK),
+            )
+        mix_ie = keep.tile([P, ROWS_PER_BLOCK, EXPERTS], F32)
+        group_softmax(
+            nc,
+            work,
+            logit_blocks[:].rearrange("p i e -> p (i e)"),
+            mix_ie[:].rearrange("p i e -> p (i e)"),
+            ROWS_PER_BLOCK * EXPERTS,
+        )
+        mix_ei = keep.tile([P, EXPERTS, ROWS_PER_BLOCK], F32)
+        nc.vector.tensor_copy(out=mix_ei[:], in_=mix_ie[:].rearrange("p i e -> p e i"))
+        mix_ps = psum.tile([P, P], F32, tag="sum")
+        nc.tensor.transpose(mix_ps[:], mix_ei[:].rearrange("p e i -> p (e i)"), identity[:])
+        mix_nj = keep.tile([P, AGENTS, BLOCKS], F32)
+        nc.scalar.copy(out=mix_nj[:].rearrange("p n j -> p (n j)"), in_=mix_ps[:])
+        same_row = keep.tile([P, ROWS_PER_BLOCK], F32)
+        nc.vector.tensor_reduce(
+            out=same_row[:],
+            in_=identity[:].rearrange("p (e i) -> p i e", i=ROWS_PER_BLOCK),
+            axis=AXIS.X,
+            op=ALU.add,
+        )
+        block_shape = [P, BLOCKS, ROWS_PER_BLOCK, AGENTS]
+        mix_blocks = keep.tile(block_shape, F32)
+        nc.gpsimd.tensor_tensor(
+            out=mix_blocks[:],
+            in0=mix_nj[:].rearrange("p n j -> p j n").unsqueeze(2).to_broadcast(block_shape),
+            in1=same_row[:].unsqueeze(1).unsqueeze(3).to_broadcast(block_shape),
+            op=ALU.mult,
+        )
+
+        h_words = keep.tile([P, EXPERTS, PASSES, BATCH], U32, align_bytes=64)
+        h_scales = keep.tile([P, EXPERTS, PASSES, BATCH], U8, align_bytes=64)
+        zT_blocks = keep.tile([P, TENSOR_CHUNKS, BLOCKS, EXPERTS, ROWS_PER_BLOCK], F32)
+        zT_rows = keep.tile([P, EXPERTS, BATCH], F32)
+
+        def quantise_expert(e):
+            grouped = work.tile([P, PASSES, BATCH, PACK], BF16, align_bytes=64)
+            for g in range(PASSES):
+                pairs_ps = psum.tile([P, 2, BATCH], F32, tag="pairs")
+                for t in range(ROW_TILES):
+                    pairs = h2_rows[:, t, e, :].bitcast(F32)
+                    for u in range(2):
+                        nc.tensor.transpose(
+                            pairs_ps[:, u, t * P : (t + 1) * P],
+                            pairs[:, g * 2 * P + u : (g + 1) * 2 * P : 2],
+                            identity[:],
+                        )
+                nc.scalar.copy(
+                    out=grouped[:, g, :, :]
+                    .rearrange("p b k -> p (b k)")
+                    .bitcast(F32)
+                    .rearrange("p (b u) -> p b u", u=2),
+                    in_=pairs_ps[:].rearrange("p u b -> p b u"),
+                )
+            nc.vector.quantize_mx(
+                out=h_words[:, e, :, :].rearrange("p g b -> p (g b)").bitcast(FP8X4),
+                scales=h_scales[:, e, :, :].rearrange("p g b -> p (g b)"),
+                in_=grouped[:].rearrange("p g b k -> p (g b k)"),
+            )
+
+        def expert_layer(e):
+            for c in range(CHUNKS):
+                cols = slice(c * P, (c + 1) * P)
+                zT_ps = psum.tile([P, BATCH], F32, tag="zT")
+                for g in range(PASSES):
+                    nc.tensor.matmul_mx(
+                        out=zT_ps[:],
+                        lhsT=w_words[:, e * PASSES + g, cols].bitcast(FP8X4),
+                        lhsT_scale=w_scales[:, e * PASSES + g, cols],
+                        rhs=h_words[:, e, g, :].bitcast(FP8X4),
+                        rhs_scale=h_scales[:, e, g, :],
+                        start=(g == 0),
+                        stop=(g == PASSES - 1),
+                    )
+                if c < TENSOR_CHUNKS:
+                    nc.scalar.activation(
+                        out=zT_blocks[:, c, :, e, :],
+                        in_=zT_ps[:].rearrange("p (j i) -> p j i", i=ROWS_PER_BLOCK),
+                        func=ACT.Identity,
+                        bias=bias[:, c, e : e + 1],
+                        scale=1.0,
+                    )
+                else:
+                    nc.scalar.activation(
+                        out=zT_rows[:, e, :],
+                        in_=zT_ps[:],
+                        func=ACT.Identity,
+                        bias=bias[:, c, e : e + 1],
+                        scale=1.0,
+                    )
+
+        y_rows = keep.tile([P, EXPERTS, ROW_TILES, P], F32)
+        out_rows = keep.tile([P, ROW_TILES, AGENTS, P], F32)
+        experts_per_bank = BANK // (ROW_TILES * P)
+
+        def vector_chunk(first):
+            experts = range(first, first + experts_per_bank)
+            z_ps = psum.tile([P, experts_per_bank, ROW_TILES, P], F32, tag="z")
+            for e in experts:
+                for t in range(ROW_TILES):
+                    nc.tensor.transpose(
+                        z_ps[:, e - first, t, :], zT_rows[:, e, t * P : (t + 1) * P], identity[:]
+                    )
+            group_softmax(
+                nc,
+                work,
+                z_ps[:].rearrange("p e t l -> p (e t l)"),
+                y_rows[:, first : first + experts_per_bank, :, :].rearrange("p e t l -> p (e t l)"),
+                BANK,
+            )
+            for e in experts:
+                for t in range(ROW_TILES):
+                    for n in range(AGENTS):
+                        if e == 0:
+                            nc.vector.tensor_scalar_mul(
+                                out=out_rows[:, t, n, :],
+                                in0=y_rows[:, e, t, :],
+                                scalar1=mix_rows[:, t, n, e : e + 1],
+                            )
+                        else:
+                            nc.vector.scalar_tensor_tensor(
+                                out=out_rows[:, t, n, :],
+                                in0=y_rows[:, e, t, :],
+                                scalar=mix_rows[:, t, n, e : e + 1],
+                                in1=out_rows[:, t, n, :],
+                                op0=ALU.mult,
+                                op1=ALU.add,
+                            )
+
+        out_flat = out.rearrange("b n l -> (b n) l")
+        blocks_per_bank = BANK // TENSOR_COLS
+
+        def tensor_chunks(first):
+            blocks = range(first, first + blocks_per_bank)
+            z_ps = psum.tile([P, blocks_per_bank, TENSOR_CHUNKS, P], F32, tag="z")
+            for j in blocks:
+                for c in range(TENSOR_CHUNKS):
+                    nc.tensor.transpose(
+                        z_ps[:, j - first, c, :],
+                        zT_blocks[:, c, j, :, :].rearrange("p e i -> p (e i)"),
+                        identity[:],
+                    )
+            y_blocks = work.tile([P, blocks_per_bank, TENSOR_COLS], F32)
+            group_softmax(
+                nc,
+                work,
+                z_ps[:].rearrange("p j c l -> p (j c l)"),
+                y_blocks[:].rearrange("p j l -> p (j l)"),
+                BANK,
+            )
+            sum_ps = psum.tile([P, blocks_per_bank, TENSOR_COLS], F32, tag="sum")
+            for j in blocks:
+                nc.tensor.matmul(
+                    out=sum_ps[:, j - first, :],
+                    lhsT=mix_blocks[:, j, :, :].rearrange("p i n -> p (i n)"),
+                    rhs=y_blocks[:, j - first, :],
+                    start=True,
+                    stop=True,
+                )
+            out_blocks = work.tile([P, blocks_per_bank, TENSOR_COLS], F32)
+            nc.scalar.copy(out=out_blocks[:], in_=sum_ps[:])
+            nc.sync.dma_start(
+                out=out_flat[first * P : (first + blocks_per_bank) * P, 0:TENSOR_COLS].rearrange(
+                    "(j m) l -> m j l", m=P
+                ),
+                in_=out_blocks[:],
+            )
+
+        quantise_expert(0)
+        for e in range(EXPERTS):
+            if e + 1 < EXPERTS:
+                quantise_expert(e + 1)
+            expert_layer(e)
+            if (e + 1) % experts_per_bank == 0:
+                vector_chunk(e + 1 - experts_per_bank)
+        for first in range(0, BLOCKS, blocks_per_bank):
+            tensor_chunks(first)
+        for t in range(ROW_TILES):
+            nc.sync.dma_start(
+                out=out[t * P : (t + 1) * P, :, TENSOR_COLS:COLS], in_=out_rows[:, t, :, :]
+            )

@@ -37,35 +37,25 @@ BLOCKS = BATCH // ROWS_PER_BLOCK
 FLOPS = 2 * BATCH * EXPERTS * FEATURES * COLS + 2 * BATCH * AGENTS * EXPERTS * COLS
 
 
-def group_softmax(nc, work, z, y, width):
-    groups = width // GROUP
-    shape = [P, groups, GROUP]
-    z_groups = z.rearrange("p (g i) -> p g i", i=GROUP)
-    top = work.tile([P, groups], F32)
-    nc.vector.tensor_reduce(out=top[:], in_=z_groups, axis=AXIS.X, op=ALU.max)
-    powers = work.tile(shape, F32)
-    nc.vector.tensor_tensor(
-        out=powers[:], in0=z_groups, in1=top[:].unsqueeze(2).to_broadcast(shape), op=ALU.subtract
-    )
-    nc.scalar.activation(out=powers[:], in_=powers[:], func=ACT.Exp)
-    total = work.tile([P, groups], F32)
-    nc.vector.tensor_reduce(out=total[:], in_=powers[:], axis=AXIS.X, op=ALU.add)
-    inverse = work.tile([P, groups], F32)
-    nc.vector.reciprocal(out=inverse[:], in_=total[:])
-    nc.gpsimd.tensor_tensor(
-        out=y.rearrange("p (g i) -> p g i", i=GROUP),
-        in0=powers[:],
-        in1=inverse[:].unsqueeze(2).to_broadcast(shape),
-        op=ALU.mult,
-    )
-
-
 def tile_softmoedynamics_pb_e_kernel(tc, h2, logits, W3_words, W3_scales, b3, out):
     nc = tc.nc
     with ExitStack() as ctx:
         keep = ctx.enter_context(tc.tile_pool(name="keep", bufs=1))
-        work = ctx.enter_context(tc.tile_pool(name="work", bufs=3))
-        psum = ctx.enter_context(tc.psum_pool(name="psum", bufs=2))
+        work = ctx.enter_context(tc.tile_pool(name="work", bufs=4))
+        psum = ctx.enter_context(tc.psum_pool(name="psum", bufs=4))
+        ctx.enter_context(tc.manual_schedule())
+
+        b3_rows = keep.tile([P, COLS], BF16)
+        nc.vector.memset(b3_rows[:], 0.0)
+        nc.scalar.dma_start(out=b3_rows[0:EXPERTS, :], in_=b3[:, :])
+        logit_rows = keep.tile([P, ROW_TILES, AGENTS * EXPERTS], BF16)
+        nc.scalar.dma_start(
+            out=logit_rows[:], in_=logits.rearrange("(t b) n e -> b t (n e)", b=P)
+        )
+        logit_blocks = keep.tile([P, ROWS_PER_BLOCK, EXPERTS], BF16)
+        nc.scalar.dma_start(
+            out=logit_blocks[:], in_=logits.rearrange("(i j) n e -> (j n) i e", j=BLOCKS)
+        )
 
         h2_rows = keep.tile([P, ROW_TILES, EXPERTS, FEATURES], BF16)
         w_words = keep.tile([P, EXPERTS * PASSES, COLS], U32, align_bytes=64)
@@ -83,6 +73,7 @@ def tile_softmoedynamics_pb_e_kernel(tc, h2, logits, W3_words, W3_scales, b3, ou
             )
 
         load_expert(0)
+        load_expert(1)
         for quadrant in range(4):
             nc.sync.dma_start(
                 out=w_scales[32 * quadrant : 32 * quadrant + 4, :, :].bitcast(I32),
@@ -90,71 +81,104 @@ def tile_softmoedynamics_pb_e_kernel(tc, h2, logits, W3_words, W3_scales, b3, ou
                 .rearrange("g r n -> r g n")
                 .bitcast(I32),
             )
-        for e in range(1, EXPERTS):
+        for e in range(2, EXPERTS):
             load_expert(e)
+
+        warm = keep.tile([P, 1], F32)
+        nc.vector.memset(warm[:], 0.0)
+        nc.scalar.activation(out=warm[:], in_=warm[:], func=ACT.Exp)
 
         identity = keep.tile([P, P], F32)
         make_identity(nc, identity[:])
 
-        b3_rows = keep.tile([P, COLS], BF16)
-        nc.vector.memset(b3_rows[:], 0.0)
-        nc.scalar.dma_start(out=b3_rows[0:EXPERTS, :], in_=b3[:, :])
         b3_wide = keep.tile([P, COLS], F32)
         nc.vector.tensor_copy(out=b3_wide[:], in_=b3_rows[:])
-        b3_ps = psum.tile([P, CHUNKS, P], F32, tag="sum")
-        for c in range(CHUNKS):
-            nc.tensor.transpose(b3_ps[:, c, :], b3_wide[:, c * P : (c + 1) * P], identity[:])
+
+        z_of = {}
+        y_of = {}
+        powers_of = {}
+        inverse_of = {}
+
+        def by_group(ap):
+            return ap.rearrange("p (g i) -> p g i", i=GROUP)
+
+        def over_group(ap):
+            return ap.unsqueeze(2).to_broadcast([P, ap.shape[1], GROUP])
+
+        def softmax_step(new=None, mid=None, old=None):
+            if new is not None:
+                z = by_group(z_of[new])
+                top = work.tile([P, z.shape[1]], F32)
+                nc.vector.tensor_reduce(out=top[:], in_=z, axis=AXIS.X, op=ALU.max)
+            if old is not None:
+                nc.vector.tensor_tensor(
+                    out=by_group(y_of[old]),
+                    in0=powers_of[old][:],
+                    in1=over_group(inverse_of[old][:]),
+                    op=ALU.mult,
+                )
+            if mid is not None:
+                total = work.tile([P, powers_of[mid].shape[1]], F32)
+                nc.vector.tensor_reduce(
+                    out=total[:], in_=powers_of[mid][:], axis=AXIS.X, op=ALU.add
+                )
+            if new is not None:
+                powers = work.tile([P, z.shape[1], GROUP], F32)
+                nc.vector.tensor_tensor(
+                    out=powers[:], in0=z, in1=over_group(top[:]), op=ALU.subtract
+                )
+                nc.scalar.activation(out=powers[:], in_=powers[:], func=ACT.Exp)
+                powers_of[new] = powers
+            if mid is not None:
+                inverse = work.tile([P, powers_of[mid].shape[1]], F32)
+                nc.vector.reciprocal(out=inverse[:], in_=total[:])
+                inverse_of[mid] = inverse
+
         bias = keep.tile([P, CHUNKS, EXPERTS], F32)
-        nc.vector.tensor_copy(out=bias[:], in_=b3_ps[:, :, 0:EXPERTS])
-
-        logit_rows = keep.tile([P, ROW_TILES, AGENTS * EXPERTS], BF16)
-        nc.scalar.dma_start(
-            out=logit_rows[:], in_=logits.rearrange("(t b) n e -> b t (n e)", b=P)
-        )
         mix_rows = keep.tile([P, ROW_TILES, AGENTS, EXPERTS], F32)
-        group_softmax(
-            nc,
-            work,
-            logit_rows[:].rearrange("b t c -> b (t c)"),
-            mix_rows[:].rearrange("b t n e -> b (t n e)"),
-            ROW_TILES * AGENTS * EXPERTS,
-        )
-
-        logit_blocks = keep.tile([P, ROWS_PER_BLOCK, EXPERTS], BF16)
-        for n in range(AGENTS):
-            nc.gpsimd.dma_start(
-                out=logit_blocks[n * BLOCKS : (n + 1) * BLOCKS, :, :],
-                in_=logits[:, n, :].rearrange("(j i) e -> j i e", i=ROWS_PER_BLOCK),
-            )
-        mix_ie = keep.tile([P, ROWS_PER_BLOCK, EXPERTS], F32)
-        group_softmax(
-            nc,
-            work,
-            logit_blocks[:].rearrange("p i e -> p (i e)"),
-            mix_ie[:].rearrange("p i e -> p (i e)"),
-            ROWS_PER_BLOCK * EXPERTS,
-        )
-        mix_ei = keep.tile([P, EXPERTS, ROWS_PER_BLOCK], F32)
-        nc.vector.tensor_copy(out=mix_ei[:], in_=mix_ie[:].rearrange("p i e -> p e i"))
-        mix_ps = psum.tile([P, P], F32, tag="sum")
-        nc.tensor.transpose(mix_ps[:], mix_ei[:].rearrange("p e i -> p (e i)"), identity[:])
-        mix_nj = keep.tile([P, AGENTS, BLOCKS], F32)
-        nc.scalar.copy(out=mix_nj[:].rearrange("p n j -> p (n j)"), in_=mix_ps[:])
-        same_row = keep.tile([P, ROWS_PER_BLOCK], F32)
-        nc.vector.tensor_reduce(
-            out=same_row[:],
-            in_=identity[:].rearrange("p (e i) -> p i e", i=ROWS_PER_BLOCK),
-            axis=AXIS.X,
-            op=ALU.add,
-        )
         block_shape = [P, BLOCKS, ROWS_PER_BLOCK, AGENTS]
         mix_blocks = keep.tile(block_shape, F32)
-        nc.gpsimd.tensor_tensor(
-            out=mix_blocks[:],
-            in0=mix_nj[:].rearrange("p n j -> p j n").unsqueeze(2).to_broadcast(block_shape),
-            in1=same_row[:].unsqueeze(1).unsqueeze(3).to_broadcast(block_shape),
-            op=ALU.mult,
-        )
+
+        def transpose_bias():
+            b3_ps = psum.tile([P, CHUNKS, P], F32, tag="out")
+            for c in range(CHUNKS):
+                nc.tensor.transpose(b3_ps[:, c, :], b3_wide[:, c * P : (c + 1) * P], identity[:])
+            nc.vector.tensor_copy(out=bias[:], in_=b3_ps[:, :, 0:EXPERTS])
+
+        mix_ie = keep.tile([P, ROWS_PER_BLOCK, EXPERTS], F32)
+        same_row = keep.tile([P, ROWS_PER_BLOCK], F32)
+
+        def mixing_softmaxes():
+            z_of["mix rows"] = logit_rows[:].rearrange("b t c -> b (t c)")
+            y_of["mix rows"] = mix_rows[:].rearrange("b t n e -> b (t n e)")
+            z_of["mix blocks"] = logit_blocks[:].rearrange("p i e -> p (i e)")
+            y_of["mix blocks"] = mix_ie[:].rearrange("p i e -> p (i e)")
+            softmax_step(new="mix rows")
+            softmax_step(new="mix blocks", mid="mix rows")
+            nc.vector.tensor_reduce(
+                out=same_row[:],
+                in_=identity[:].rearrange("p (e i) -> p i e", i=ROWS_PER_BLOCK),
+                axis=AXIS.X,
+                op=ALU.add,
+            )
+            softmax_step(mid="mix blocks", old="mix rows")
+            softmax_step(old="mix blocks")
+
+        def build_mix_blocks():
+            mix_ei = keep.tile([P, EXPERTS, ROWS_PER_BLOCK], F32)
+            nc.vector.tensor_copy(out=mix_ei[:], in_=mix_ie[:].rearrange("p i e -> p e i"))
+            mix_ps = psum.tile([P, BLOCKS, AGENTS], F32, tag="out")
+            nc.tensor.transpose(
+                mix_ps[:].rearrange("p j n -> p (j n)"),
+                mix_ei[:].rearrange("p e i -> p (e i)"),
+                identity[:],
+            )
+            nc.vector.tensor_tensor(
+                out=mix_blocks[:],
+                in0=mix_ps[:].unsqueeze(2).to_broadcast(block_shape),
+                in1=same_row[:].unsqueeze(1).unsqueeze(3).to_broadcast(block_shape),
+                op=ALU.mult,
+            )
 
         h_words = keep.tile([P, EXPERTS, PASSES, BATCH], U32, align_bytes=64)
         h_scales = keep.tile([P, EXPERTS, PASSES, BATCH], U8, align_bytes=64)
@@ -164,7 +188,7 @@ def tile_softmoedynamics_pb_e_kernel(tc, h2, logits, W3_words, W3_scales, b3, ou
         def quantise_expert(e):
             grouped = work.tile([P, PASSES, BATCH, PACK], BF16, align_bytes=64)
             for g in range(PASSES):
-                pairs_ps = psum.tile([P, 2, BATCH], F32, tag="pairs")
+                pairs_ps = psum.tile([P, 2, BATCH], F32, tag="in")
                 for t in range(ROW_TILES):
                     pairs = h2_rows[:, t, e, :].bitcast(F32)
                     for u in range(2):
@@ -189,7 +213,7 @@ def tile_softmoedynamics_pb_e_kernel(tc, h2, logits, W3_words, W3_scales, b3, ou
         def expert_layer(e):
             for c in range(CHUNKS):
                 cols = slice(c * P, (c + 1) * P)
-                zT_ps = psum.tile([P, BATCH], F32, tag="zT")
+                zT_ps = psum.tile([P, BATCH], F32, tag="out")
                 for g in range(PASSES):
                     nc.tensor.matmul_mx(
                         out=zT_ps[:],
@@ -203,7 +227,7 @@ def tile_softmoedynamics_pb_e_kernel(tc, h2, logits, W3_words, W3_scales, b3, ou
                 if c < TENSOR_CHUNKS:
                     nc.scalar.activation(
                         out=zT_blocks[:, c, :, e, :],
-                        in_=zT_ps[:].rearrange("p (j i) -> p j i", i=ROWS_PER_BLOCK),
+                        in_=zT_ps[:].rearrange("p (i j) -> p j i", j=BLOCKS),
                         func=ACT.Identity,
                         bias=bias[:, c, e : e + 1],
                         scale=1.0,
@@ -219,90 +243,115 @@ def tile_softmoedynamics_pb_e_kernel(tc, h2, logits, W3_words, W3_scales, b3, ou
 
         y_rows = keep.tile([P, EXPERTS, ROW_TILES, P], F32)
         out_rows = keep.tile([P, ROW_TILES, AGENTS, P], F32)
-        experts_per_bank = BANK // (ROW_TILES * P)
+        experts_per_round = BANK // (ROW_TILES * P)
+        row_rounds = EXPERTS // experts_per_round
 
-        def vector_chunk(first):
-            experts = range(first, first + experts_per_bank)
-            z_ps = psum.tile([P, experts_per_bank, ROW_TILES, P], F32, tag="z")
-            for e in experts:
+        def spread_rows(r):
+            first = r * experts_per_round
+            z_ps = psum.tile([P, experts_per_round, ROW_TILES, P], F32, tag="in")
+            for e in range(first, first + experts_per_round):
                 for t in range(ROW_TILES):
                     nc.tensor.transpose(
                         z_ps[:, e - first, t, :], zT_rows[:, e, t * P : (t + 1) * P], identity[:]
                     )
-            group_softmax(
-                nc,
-                work,
-                z_ps[:].rearrange("p e t l -> p (e t l)"),
-                y_rows[:, first : first + experts_per_bank, :, :].rearrange("p e t l -> p (e t l)"),
-                BANK,
+            z_of[("rows", r)] = z_ps[:].rearrange("p e t l -> p (e t l)")
+            y_of[("rows", r)] = y_rows[:, first : first + experts_per_round, :, :].rearrange(
+                "p e t l -> p (e t l)"
             )
-            for e in experts:
-                for t in range(ROW_TILES):
-                    for n in range(AGENTS):
-                        if e == 0:
-                            nc.vector.tensor_scalar_mul(
-                                out=out_rows[:, t, n, :],
-                                in0=y_rows[:, e, t, :],
-                                scalar1=mix_rows[:, t, n, e : e + 1],
-                            )
-                        else:
-                            nc.vector.scalar_tensor_tensor(
-                                out=out_rows[:, t, n, :],
-                                in0=y_rows[:, e, t, :],
-                                scalar=mix_rows[:, t, n, e : e + 1],
-                                in1=out_rows[:, t, n, :],
-                                op0=ALU.mult,
-                                op1=ALU.add,
-                            )
 
-        out_flat = out.rearrange("b n l -> (b n) l")
-        blocks_per_bank = BANK // TENSOR_COLS
+        def weigh_expert(e):
+            for t in range(ROW_TILES):
+                for n in range(AGENTS):
+                    if e == 0:
+                        nc.vector.tensor_scalar_mul(
+                            out=out_rows[:, t, n, :],
+                            in0=y_rows[:, e, t, :],
+                            scalar1=mix_rows[:, t, n, e : e + 1],
+                        )
+                    else:
+                        nc.vector.scalar_tensor_tensor(
+                            out=out_rows[:, t, n, :],
+                            in0=y_rows[:, e, t, :],
+                            scalar=mix_rows[:, t, n, e : e + 1],
+                            in1=out_rows[:, t, n, :],
+                            op0=ALU.mult,
+                            op1=ALU.add,
+                        )
 
-        def tensor_chunks(first):
-            blocks = range(first, first + blocks_per_bank)
-            z_ps = psum.tile([P, blocks_per_bank, TENSOR_CHUNKS, P], F32, tag="z")
-            for j in blocks:
+        out_by_block = out.rearrange("(i j) n l -> j i n l", j=BLOCKS)
+        blocks_per_round = BANK // TENSOR_COLS
+        block_rounds = BLOCKS // blocks_per_round
+        y_blocks_of = {}
+
+        def spread_blocks(r):
+            first = r * blocks_per_round
+            z_ps = psum.tile([P, blocks_per_round, TENSOR_CHUNKS, P], F32, tag="in")
+            for j in range(first, first + blocks_per_round):
                 for c in range(TENSOR_CHUNKS):
                     nc.tensor.transpose(
                         z_ps[:, j - first, c, :],
                         zT_blocks[:, c, j, :, :].rearrange("p e i -> p (e i)"),
                         identity[:],
                     )
-            y_blocks = work.tile([P, blocks_per_bank, TENSOR_COLS], F32)
-            group_softmax(
-                nc,
-                work,
-                z_ps[:].rearrange("p j c l -> p (j c l)"),
-                y_blocks[:].rearrange("p j l -> p (j l)"),
-                BANK,
-            )
-            sum_ps = psum.tile([P, blocks_per_bank, TENSOR_COLS], F32, tag="sum")
-            for j in blocks:
+            y_blocks = work.tile([P, blocks_per_round, TENSOR_COLS], F32)
+            z_of[("blocks", r)] = z_ps[:].rearrange("p j c l -> p (j c l)")
+            y_of[("blocks", r)] = y_blocks[:].rearrange("p j l -> p (j l)")
+            y_blocks_of[r] = y_blocks
+
+        def combine_blocks(r):
+            first = r * blocks_per_round
+            sum_ps = psum.tile([P, blocks_per_round, TENSOR_COLS], F32, tag="out")
+            for j in range(first, first + blocks_per_round):
                 nc.tensor.matmul(
                     out=sum_ps[:, j - first, :],
                     lhsT=mix_blocks[:, j, :, :].rearrange("p i n -> p (i n)"),
-                    rhs=y_blocks[:, j - first, :],
+                    rhs=y_blocks_of[r][:, j - first, :],
                     start=True,
                     stop=True,
                 )
-            out_blocks = work.tile([P, blocks_per_bank, TENSOR_COLS], F32)
+            out_blocks = work.tile([P, blocks_per_round, TENSOR_COLS], F32)
             nc.scalar.copy(out=out_blocks[:], in_=sum_ps[:])
-            nc.sync.dma_start(
-                out=out_flat[first * P : (first + blocks_per_bank) * P, 0:TENSOR_COLS].rearrange(
-                    "(j m) l -> m j l", m=P
-                ),
-                in_=out_blocks[:],
-            )
+            for j in range(first, first + blocks_per_round):
+                nc.sync.dma_start(
+                    out=out_by_block[j, :, :, 0:TENSOR_COLS], in_=out_blocks[:, j - first, :]
+                )
+
+        rounds = [("rows", r) for r in range(row_rounds)] + [
+            ("blocks", r) for r in range(block_rounds)
+        ]
+
+        def round_at(k):
+            return rounds[k] if 0 <= k < len(rounds) else None
+
+        def round_step(k):
+            softmax_step(new=round_at(k), mid=round_at(k - 1), old=round_at(k - 2))
 
         quantise_expert(0)
-        for e in range(EXPERTS):
-            if e + 1 < EXPERTS:
-                quantise_expert(e + 1)
+        transpose_bias()
+        quantise_expert(1)
+        mixing_softmaxes()
+        for e in range(experts_per_round):
+            quantise_expert(e + 2)
             expert_layer(e)
-            if (e + 1) % experts_per_bank == 0:
-                vector_chunk(e + 1 - experts_per_bank)
-        for first in range(0, BLOCKS, blocks_per_bank):
-            tensor_chunks(first)
+        build_mix_blocks()
+        for e in range(experts_per_round, EXPERTS):
+            if e + 2 < EXPERTS:
+                quantise_expert(e + 2)
+            expert_layer(e)
+            if e % experts_per_round == 0:
+                spread_rows(e // experts_per_round - 1)
+                round_step(e // experts_per_round - 1)
+        spread_rows(row_rounds - 1)
+        round_step(row_rounds - 1)
+
+        assert block_rounds == EXPERTS
+        for s in range(block_rounds + 2):
+            if s < block_rounds:
+                spread_blocks(s)
+            round_step(row_rounds + s)
+            if s >= 2:
+                combine_blocks(s - 2)
+                weigh_expert(s - 2)
         for t in range(ROW_TILES):
             nc.sync.dma_start(
                 out=out[t * P : (t + 1) * P, :, TENSOR_COLS:COLS], in_=out_rows[:, t, :, :]

@@ -41,7 +41,7 @@ def tile_softmoedynamics_pb_e_kernel(tc, h2, logits, W3_words, W3_scales, b3, ou
     nc = tc.nc
     with ExitStack() as ctx:
         keep = ctx.enter_context(tc.tile_pool(name="keep", bufs=1))
-        work = ctx.enter_context(tc.tile_pool(name="work", bufs=4))
+        work = ctx.enter_context(tc.tile_pool(name="work", bufs=6))
         psum = ctx.enter_context(tc.psum_pool(name="psum", bufs=4))
         ctx.enter_context(tc.manual_schedule())
 
@@ -57,7 +57,7 @@ def tile_softmoedynamics_pb_e_kernel(tc, h2, logits, W3_words, W3_scales, b3, ou
             out=logit_blocks[:], in_=logits.rearrange("(i j) n e -> (j n) i e", j=BLOCKS)
         )
 
-        h2_rows = keep.tile([P, ROW_TILES, EXPERTS, FEATURES], BF16)
+        h2_rows = keep.tile([P, EXPERTS, ROW_TILES, FEATURES], BF16)
         w_words = keep.tile([P, EXPERTS * PASSES, COLS], U32, align_bytes=64)
         w_scales = keep.tile([P, EXPERTS * PASSES, COLS], U8, align_bytes=64)
         nc.vector.memset(w_scales[:].bitcast(I32), 0)
@@ -65,7 +65,7 @@ def tile_softmoedynamics_pb_e_kernel(tc, h2, logits, W3_words, W3_scales, b3, ou
         def load_expert(e):
             passes = slice(e * PASSES, (e + 1) * PASSES)
             nc.sync.dma_start(
-                out=h2_rows[:, :, e, :], in_=h2[:, e, :].rearrange("(t b) k -> b t k", b=P)
+                out=h2_rows[:, e, :, :], in_=h2[:, e, :].rearrange("(t b) k -> b t k", b=P)
             )
             nc.sync.dma_start(
                 out=w_words[:, passes, :].bitcast(I32),
@@ -94,9 +94,11 @@ def tile_softmoedynamics_pb_e_kernel(tc, h2, logits, W3_words, W3_scales, b3, ou
         b3_wide = keep.tile([P, COLS], F32)
         nc.vector.tensor_copy(out=b3_wide[:], in_=b3_rows[:])
 
+        STAGES = 4
         z_of = {}
         y_of = {}
         powers_of = {}
+        total_of = {}
         inverse_of = {}
 
         def by_group(ap):
@@ -105,34 +107,51 @@ def tile_softmoedynamics_pb_e_kernel(tc, h2, logits, W3_words, W3_scales, b3, ou
         def over_group(ap):
             return ap.unsqueeze(2).to_broadcast([P, ap.shape[1], GROUP])
 
-        def softmax_step(new=None, mid=None, old=None):
-            if new is not None:
-                z = by_group(z_of[new])
+        def softmax_step(first, second, third, fourth):
+            if first is not None:
+                z = by_group(z_of[first])
                 top = work.tile([P, z.shape[1]], F32)
                 nc.vector.tensor_reduce(out=top[:], in_=z, axis=AXIS.X, op=ALU.max)
-            if old is not None:
-                nc.vector.tensor_tensor(
-                    out=by_group(y_of[old]),
-                    in0=powers_of[old][:],
-                    in1=over_group(inverse_of[old][:]),
-                    op=ALU.mult,
-                )
-            if mid is not None:
-                total = work.tile([P, powers_of[mid].shape[1]], F32)
-                nc.vector.tensor_reduce(
-                    out=total[:], in_=powers_of[mid][:], axis=AXIS.X, op=ALU.add
-                )
-            if new is not None:
+            if third is not None:
+                inverse = work.tile([P, total_of[third].shape[1]], F32)
+                nc.vector.reciprocal(out=inverse[:], in_=total_of[third][:, :, 0])
+                inverse_of[third] = inverse
+            if first is not None:
                 powers = work.tile([P, z.shape[1], GROUP], F32)
                 nc.vector.tensor_tensor(
                     out=powers[:], in0=z, in1=over_group(top[:]), op=ALU.subtract
                 )
                 nc.scalar.activation(out=powers[:], in_=powers[:], func=ACT.Exp)
-                powers_of[new] = powers
-            if mid is not None:
-                inverse = work.tile([P, powers_of[mid].shape[1]], F32)
-                nc.vector.reciprocal(out=inverse[:], in_=total[:])
-                inverse_of[mid] = inverse
+                powers_of[first] = powers
+            if second is not None:
+                summed = powers_of[second]
+                fours = work.tile([P, summed.shape[1], 4], F32)
+                nc.gpsimd.tensor_tensor(
+                    out=fours[:], in0=summed[:, :, 0:4], in1=summed[:, :, 4:8], op=ALU.add
+                )
+            if fourth is not None:
+                nc.gpsimd.tensor_tensor(
+                    out=by_group(y_of[fourth]),
+                    in0=powers_of[fourth][:],
+                    in1=over_group(inverse_of[fourth][:]),
+                    op=ALU.mult,
+                )
+            if second is not None:
+                twos = work.tile([P, summed.shape[1], 2], F32)
+                nc.gpsimd.tensor_tensor(
+                    out=twos[:], in0=fours[:, :, 0:2], in1=fours[:, :, 2:4], op=ALU.add
+                )
+                total = work.tile([P, summed.shape[1], 1], F32)
+                nc.gpsimd.tensor_tensor(
+                    out=total[:], in0=twos[:, :, 0:1], in1=twos[:, :, 1:2], op=ALU.add
+                )
+                total_of[second] = total
+
+        def step_of(names, k):
+            in_stage = [
+                names[k - lag] if 0 <= k - lag < len(names) else None for lag in range(STAGES)
+            ]
+            softmax_step(*in_stage)
 
         bias = keep.tile([P, CHUNKS, EXPERTS], F32)
         mix_rows = keep.tile([P, ROW_TILES, AGENTS, EXPERTS], F32)
@@ -148,23 +167,19 @@ def tile_softmoedynamics_pb_e_kernel(tc, h2, logits, W3_words, W3_scales, b3, ou
         mix_ie = keep.tile([P, ROWS_PER_BLOCK, EXPERTS], F32)
         same_row = keep.tile([P, ROWS_PER_BLOCK], F32)
 
-        def mixing_softmaxes():
-            z_of["mix rows"] = logit_rows[:].rearrange("b t c -> b (t c)")
-            y_of["mix rows"] = mix_rows[:].rearrange("b t n e -> b (t n e)")
-            z_of["mix blocks"] = logit_blocks[:].rearrange("p i e -> p (i e)")
-            y_of["mix blocks"] = mix_ie[:].rearrange("p i e -> p (i e)")
-            softmax_step(new="mix rows")
-            softmax_step(new="mix blocks", mid="mix rows")
+        mix_rounds = ["mix rows", "mix blocks"]
+        z_of["mix rows"] = logit_rows[:].rearrange("b t c -> b (t c)")
+        y_of["mix rows"] = mix_rows[:].rearrange("b t n e -> b (t n e)")
+        z_of["mix blocks"] = logit_blocks[:].rearrange("p i e -> p (i e)")
+        y_of["mix blocks"] = mix_ie[:].rearrange("p i e -> p (i e)")
+
+        def build_mix_blocks():
             nc.vector.tensor_reduce(
                 out=same_row[:],
                 in_=identity[:].rearrange("p (e i) -> p i e", i=ROWS_PER_BLOCK),
                 axis=AXIS.X,
                 op=ALU.add,
             )
-            softmax_step(mid="mix blocks", old="mix rows")
-            softmax_step(old="mix blocks")
-
-        def build_mix_blocks():
             mix_ei = keep.tile([P, EXPERTS, ROWS_PER_BLOCK], F32)
             nc.vector.tensor_copy(out=mix_ei[:], in_=mix_ie[:].rearrange("p i e -> p e i"))
             mix_ps = psum.tile([P, BLOCKS, AGENTS], F32, tag="out")
@@ -173,9 +188,11 @@ def tile_softmoedynamics_pb_e_kernel(tc, h2, logits, W3_words, W3_scales, b3, ou
                 mix_ei[:].rearrange("p e i -> p (e i)"),
                 identity[:],
             )
-            nc.vector.tensor_tensor(
+            mix_jn = keep.tile([P, BLOCKS, AGENTS], F32)
+            nc.scalar.copy(out=mix_jn[:], in_=mix_ps[:])
+            nc.gpsimd.tensor_tensor(
                 out=mix_blocks[:],
-                in0=mix_ps[:].unsqueeze(2).to_broadcast(block_shape),
+                in0=mix_jn[:].unsqueeze(2).to_broadcast(block_shape),
                 in1=same_row[:].unsqueeze(1).unsqueeze(3).to_broadcast(block_shape),
                 op=ALU.mult,
             )
@@ -190,7 +207,7 @@ def tile_softmoedynamics_pb_e_kernel(tc, h2, logits, W3_words, W3_scales, b3, ou
             for g in range(PASSES):
                 pairs_ps = psum.tile([P, 2, BATCH], F32, tag="in")
                 for t in range(ROW_TILES):
-                    pairs = h2_rows[:, t, e, :].bitcast(F32)
+                    pairs = h2_rows[:, e, t, :].bitcast(F32)
                     for u in range(2):
                         nc.tensor.transpose(
                             pairs_ps[:, u, t * P : (t + 1) * P],
@@ -316,41 +333,37 @@ def tile_softmoedynamics_pb_e_kernel(tc, h2, logits, W3_words, W3_scales, b3, ou
                     out=out_by_block[j, :, :, 0:TENSOR_COLS], in_=out_blocks[:, j - first, :]
                 )
 
-        rounds = [("rows", r) for r in range(row_rounds)] + [
-            ("blocks", r) for r in range(block_rounds)
-        ]
-
-        def round_at(k):
-            return rounds[k] if 0 <= k < len(rounds) else None
-
-        def round_step(k):
-            softmax_step(new=round_at(k), mid=round_at(k - 1), old=round_at(k - 2))
+        rounds = (
+            mix_rounds
+            + [("rows", r) for r in range(row_rounds)]
+            + [("blocks", r) for r in range(block_rounds)]
+        )
+        first_rows = len(mix_rounds)
+        first_blocks = first_rows + row_rounds
 
         quantise_expert(0)
         transpose_bias()
         quantise_expert(1)
-        mixing_softmaxes()
-        for e in range(experts_per_round):
-            quantise_expert(e + 2)
-            expert_layer(e)
-        build_mix_blocks()
-        for e in range(experts_per_round, EXPERTS):
+        for k in range(first_rows):
+            step_of(rounds, k)
+        for e in range(EXPERTS):
             if e + 2 < EXPERTS:
                 quantise_expert(e + 2)
             expert_layer(e)
-            if e % experts_per_round == 0:
+            if e >= experts_per_round and e % experts_per_round == 0:
                 spread_rows(e // experts_per_round - 1)
-                round_step(e // experts_per_round - 1)
+                step_of(rounds, first_rows + e // experts_per_round - 1)
         spread_rows(row_rounds - 1)
-        round_step(row_rounds - 1)
+        step_of(rounds, first_blocks - 1)
+        build_mix_blocks()
 
-        assert block_rounds == EXPERTS
-        for s in range(block_rounds + 2):
+        for s in range(block_rounds + STAGES):
             if s < block_rounds:
                 spread_blocks(s)
-            round_step(row_rounds + s)
-            if s >= 2:
-                combine_blocks(s - 2)
+            step_of(rounds, first_blocks + s)
+            if s >= STAGES:
+                combine_blocks(s - STAGES)
+            if 2 <= s < EXPERTS + 2:
                 weigh_expert(s - 2)
         for t in range(ROW_TILES):
             nc.sync.dma_start(

@@ -41,7 +41,7 @@ def tile_softmoedynamics_pb_e_kernel(tc, h2, logits, W3_words, W3_scales, b3, ou
     nc = tc.nc
     with ExitStack() as ctx:
         keep = ctx.enter_context(tc.tile_pool(name="keep", bufs=1))
-        work = ctx.enter_context(tc.tile_pool(name="work", bufs=6))
+        work = ctx.enter_context(tc.tile_pool(name="work", bufs=4))
         psum = ctx.enter_context(tc.psum_pool(name="psum", bufs=4))
         ctx.enter_context(tc.manual_schedule())
 
@@ -94,11 +94,9 @@ def tile_softmoedynamics_pb_e_kernel(tc, h2, logits, W3_words, W3_scales, b3, ou
         b3_wide = keep.tile([P, COLS], F32)
         nc.vector.tensor_copy(out=b3_wide[:], in_=b3_rows[:])
 
-        STAGES = 4
         z_of = {}
         y_of = {}
         powers_of = {}
-        total_of = {}
         inverse_of = {}
 
         def by_group(ap):
@@ -107,51 +105,34 @@ def tile_softmoedynamics_pb_e_kernel(tc, h2, logits, W3_words, W3_scales, b3, ou
         def over_group(ap):
             return ap.unsqueeze(2).to_broadcast([P, ap.shape[1], GROUP])
 
-        def softmax_step(first, second, third, fourth):
-            if first is not None:
-                z = by_group(z_of[first])
+        def softmax_step(new=None, mid=None, old=None):
+            if new is not None:
+                z = by_group(z_of[new])
                 top = work.tile([P, z.shape[1]], F32)
                 nc.vector.tensor_reduce(out=top[:], in_=z, axis=AXIS.X, op=ALU.max)
-            if third is not None:
-                inverse = work.tile([P, total_of[third].shape[1]], F32)
-                nc.vector.reciprocal(out=inverse[:], in_=total_of[third][:, :, 0])
-                inverse_of[third] = inverse
-            if first is not None:
+            if old is not None:
+                nc.vector.tensor_tensor(
+                    out=by_group(y_of[old]),
+                    in0=powers_of[old][:],
+                    in1=over_group(inverse_of[old][:]),
+                    op=ALU.mult,
+                )
+            if mid is not None:
+                total = work.tile([P, powers_of[mid].shape[1]], F32)
+                nc.vector.tensor_reduce(
+                    out=total[:], in_=powers_of[mid][:], axis=AXIS.X, op=ALU.add
+                )
+            if new is not None:
                 powers = work.tile([P, z.shape[1], GROUP], F32)
                 nc.vector.tensor_tensor(
                     out=powers[:], in0=z, in1=over_group(top[:]), op=ALU.subtract
                 )
                 nc.scalar.activation(out=powers[:], in_=powers[:], func=ACT.Exp)
-                powers_of[first] = powers
-            if second is not None:
-                summed = powers_of[second]
-                fours = work.tile([P, summed.shape[1], 4], F32)
-                nc.gpsimd.tensor_tensor(
-                    out=fours[:], in0=summed[:, :, 0:4], in1=summed[:, :, 4:8], op=ALU.add
-                )
-            if fourth is not None:
-                nc.gpsimd.tensor_tensor(
-                    out=by_group(y_of[fourth]),
-                    in0=powers_of[fourth][:],
-                    in1=over_group(inverse_of[fourth][:]),
-                    op=ALU.mult,
-                )
-            if second is not None:
-                twos = work.tile([P, summed.shape[1], 2], F32)
-                nc.gpsimd.tensor_tensor(
-                    out=twos[:], in0=fours[:, :, 0:2], in1=fours[:, :, 2:4], op=ALU.add
-                )
-                total = work.tile([P, summed.shape[1], 1], F32)
-                nc.gpsimd.tensor_tensor(
-                    out=total[:], in0=twos[:, :, 0:1], in1=twos[:, :, 1:2], op=ALU.add
-                )
-                total_of[second] = total
-
-        def step_of(names, k):
-            in_stage = [
-                names[k - lag] if 0 <= k - lag < len(names) else None for lag in range(STAGES)
-            ]
-            softmax_step(*in_stage)
+                powers_of[new] = powers
+            if mid is not None:
+                inverse = work.tile([P, powers_of[mid].shape[1]], F32)
+                nc.vector.reciprocal(out=inverse[:], in_=total[:])
+                inverse_of[mid] = inverse
 
         bias = keep.tile([P, CHUNKS, EXPERTS], F32)
         mix_rows = keep.tile([P, ROW_TILES, AGENTS, EXPERTS], F32)
@@ -167,19 +148,23 @@ def tile_softmoedynamics_pb_e_kernel(tc, h2, logits, W3_words, W3_scales, b3, ou
         mix_ie = keep.tile([P, ROWS_PER_BLOCK, EXPERTS], F32)
         same_row = keep.tile([P, ROWS_PER_BLOCK], F32)
 
-        mix_rounds = ["mix rows", "mix blocks"]
-        z_of["mix rows"] = logit_rows[:].rearrange("b t c -> b (t c)")
-        y_of["mix rows"] = mix_rows[:].rearrange("b t n e -> b (t n e)")
-        z_of["mix blocks"] = logit_blocks[:].rearrange("p i e -> p (i e)")
-        y_of["mix blocks"] = mix_ie[:].rearrange("p i e -> p (i e)")
-
-        def build_mix_blocks():
+        def mixing_softmaxes():
+            z_of["mix rows"] = logit_rows[:].rearrange("b t c -> b (t c)")
+            y_of["mix rows"] = mix_rows[:].rearrange("b t n e -> b (t n e)")
+            z_of["mix blocks"] = logit_blocks[:].rearrange("p i e -> p (i e)")
+            y_of["mix blocks"] = mix_ie[:].rearrange("p i e -> p (i e)")
+            softmax_step(new="mix rows")
+            softmax_step(new="mix blocks", mid="mix rows")
             nc.vector.tensor_reduce(
                 out=same_row[:],
                 in_=identity[:].rearrange("p (e i) -> p i e", i=ROWS_PER_BLOCK),
                 axis=AXIS.X,
                 op=ALU.add,
             )
+            softmax_step(mid="mix blocks", old="mix rows")
+            softmax_step(old="mix blocks")
+
+        def build_mix_blocks():
             mix_ei = keep.tile([P, EXPERTS, ROWS_PER_BLOCK], F32)
             nc.vector.tensor_copy(out=mix_ei[:], in_=mix_ie[:].rearrange("p i e -> p e i"))
             mix_ps = psum.tile([P, BLOCKS, AGENTS], F32, tag="out")
@@ -188,11 +173,9 @@ def tile_softmoedynamics_pb_e_kernel(tc, h2, logits, W3_words, W3_scales, b3, ou
                 mix_ei[:].rearrange("p e i -> p (e i)"),
                 identity[:],
             )
-            mix_jn = keep.tile([P, BLOCKS, AGENTS], F32)
-            nc.scalar.copy(out=mix_jn[:], in_=mix_ps[:])
-            nc.gpsimd.tensor_tensor(
+            nc.vector.tensor_tensor(
                 out=mix_blocks[:],
-                in0=mix_jn[:].unsqueeze(2).to_broadcast(block_shape),
+                in0=mix_ps[:].unsqueeze(2).to_broadcast(block_shape),
                 in1=same_row[:].unsqueeze(1).unsqueeze(3).to_broadcast(block_shape),
                 op=ALU.mult,
             )
@@ -333,37 +316,41 @@ def tile_softmoedynamics_pb_e_kernel(tc, h2, logits, W3_words, W3_scales, b3, ou
                     out=out_by_block[j, :, :, 0:TENSOR_COLS], in_=out_blocks[:, j - first, :]
                 )
 
-        rounds = (
-            mix_rounds
-            + [("rows", r) for r in range(row_rounds)]
-            + [("blocks", r) for r in range(block_rounds)]
-        )
-        first_rows = len(mix_rounds)
-        first_blocks = first_rows + row_rounds
+        rounds = [("rows", r) for r in range(row_rounds)] + [
+            ("blocks", r) for r in range(block_rounds)
+        ]
+
+        def round_at(k):
+            return rounds[k] if 0 <= k < len(rounds) else None
+
+        def round_step(k):
+            softmax_step(new=round_at(k), mid=round_at(k - 1), old=round_at(k - 2))
 
         quantise_expert(0)
         transpose_bias()
         quantise_expert(1)
-        for k in range(first_rows):
-            step_of(rounds, k)
-        for e in range(EXPERTS):
+        mixing_softmaxes()
+        for e in range(experts_per_round):
+            quantise_expert(e + 2)
+            expert_layer(e)
+        build_mix_blocks()
+        for e in range(experts_per_round, EXPERTS):
             if e + 2 < EXPERTS:
                 quantise_expert(e + 2)
             expert_layer(e)
-            if e >= experts_per_round and e % experts_per_round == 0:
+            if e % experts_per_round == 0:
                 spread_rows(e // experts_per_round - 1)
-                step_of(rounds, first_rows + e // experts_per_round - 1)
+                round_step(e // experts_per_round - 1)
         spread_rows(row_rounds - 1)
-        step_of(rounds, first_blocks - 1)
-        build_mix_blocks()
+        round_step(row_rounds - 1)
 
-        for s in range(block_rounds + STAGES):
+        assert block_rounds == EXPERTS
+        for s in range(block_rounds + 2):
             if s < block_rounds:
                 spread_blocks(s)
-            step_of(rounds, first_blocks + s)
-            if s >= STAGES:
-                combine_blocks(s - STAGES)
-            if 2 <= s < EXPERTS + 2:
+            round_step(row_rounds + s)
+            if s >= 2:
+                combine_blocks(s - 2)
                 weigh_expert(s - 2)
         for t in range(ROW_TILES):
             nc.sync.dma_start(

@@ -16,6 +16,7 @@ AXIS = mybir.AxisListType
 P = 128
 PACK = 4
 K_PASS = P * PACK
+BANK = 512
 
 BATCH = 256
 EXPERTS = 8
@@ -27,14 +28,22 @@ GROUP = 8
 PASSES = FEATURES // K_PASS
 ROW_TILES = BATCH // P
 CHUNKS = COLS // P
-BANK = 512
 
-TENSOR_CHUNKS = 2
-TENSOR_COLS = TENSOR_CHUNKS * P
+MX_FLOPS = 2 * BATCH * EXPERTS * FEATURES * COLS
+FLOPS = MX_FLOPS + 2 * BATCH * AGENTS * EXPERTS * COLS
+
 ROWS_PER_BLOCK = P // EXPERTS
 BLOCKS = BATCH // ROWS_PER_BLOCK
+BLOCKS_PER_TILE = P // ROWS_PER_BLOCK
+VECTOR_COLS = 160
+assert 10 * (2 * P * AGENTS * (BATCH * COLS - P * VECTOR_COLS)) <= MX_FLOPS
+VECTOR_FIRST = COLS - VECTOR_COLS
+VECTOR_CHUNK = VECTOR_FIRST // P
 
-FLOPS = 2 * BATCH * EXPERTS * FEATURES * COLS + 2 * BATCH * AGENTS * EXPERTS * COLS
+
+def tensor_width(c, t):
+    last = COLS if t < ROW_TILES - 1 else VECTOR_FIRST
+    return max(0, min(P, last - c * P))
 
 
 def tile_softmoedynamics_pb_e_kernel(tc, h2, logits, W3_words, W3_scales, b3, out):
@@ -48,13 +57,9 @@ def tile_softmoedynamics_pb_e_kernel(tc, h2, logits, W3_words, W3_scales, b3, ou
         b3_rows = keep.tile([P, COLS], BF16)
         nc.vector.memset(b3_rows[:], 0.0)
         nc.scalar.dma_start(out=b3_rows[0:EXPERTS, :], in_=b3[:, :])
-        logit_rows = keep.tile([P, ROW_TILES, AGENTS * EXPERTS], BF16)
+        logit_rows = keep.tile([P, 1, AGENTS * EXPERTS], BF16)
         nc.scalar.dma_start(
-            out=logit_rows[:], in_=logits.rearrange("(t b) n e -> b t (n e)", b=P)
-        )
-        logit_blocks = keep.tile([P, ROWS_PER_BLOCK, EXPERTS], BF16)
-        nc.scalar.dma_start(
-            out=logit_blocks[:], in_=logits.rearrange("(i j) n e -> (j n) i e", j=BLOCKS)
+            out=logit_rows[:, 0, :], in_=logits[BATCH - P : BATCH].rearrange("b n e -> b (n e)")
         )
 
         h2_rows = keep.tile([P, EXPERTS, ROW_TILES, FEATURES], BF16)
@@ -83,6 +88,14 @@ def tile_softmoedynamics_pb_e_kernel(tc, h2, logits, W3_words, W3_scales, b3, ou
             )
         for e in range(2, EXPERTS):
             load_expert(e)
+        logit_blocks = keep.tile([P, 1, ROWS_PER_BLOCK * EXPERTS], BF16)
+        for n in range(AGENTS):
+            nc.sync.dma_start(
+                out=logit_blocks[n * BLOCKS : (n + 1) * BLOCKS, 0, :].rearrange(
+                    "j (i e) -> j i e", e=EXPERTS
+                ),
+                in_=logits[:, n, :].rearrange("(j i) e -> j i e", i=ROWS_PER_BLOCK),
+            )
 
         warm = keep.tile([P, 1], F32)
         nc.vector.memset(warm[:], 0.0)
@@ -100,15 +113,15 @@ def tile_softmoedynamics_pb_e_kernel(tc, h2, logits, W3_words, W3_scales, b3, ou
         inverse_of = {}
 
         def by_group(ap):
-            return ap.rearrange("p (g i) -> p g i", i=GROUP)
+            return ap.rearrange("p a (g i) -> p a g i", i=GROUP)
 
         def over_group(ap):
-            return ap.unsqueeze(2).to_broadcast([P, ap.shape[1], GROUP])
+            return ap.unsqueeze(3).to_broadcast([P, ap.shape[1], ap.shape[2], GROUP])
 
-        def softmax_step(new=None, mid=None, old=None):
+        def softmax_step(new, mid, old):
             if new is not None:
                 z = by_group(z_of[new])
-                top = work.tile([P, z.shape[1]], F32)
+                top = work.tile([P, z.shape[1], z.shape[2]], F32)
                 nc.vector.tensor_reduce(out=top[:], in_=z, axis=AXIS.X, op=ALU.max)
             if old is not None:
                 nc.vector.tensor_tensor(
@@ -118,26 +131,22 @@ def tile_softmoedynamics_pb_e_kernel(tc, h2, logits, W3_words, W3_scales, b3, ou
                     op=ALU.mult,
                 )
             if mid is not None:
-                total = work.tile([P, powers_of[mid].shape[1]], F32)
-                nc.vector.tensor_reduce(
-                    out=total[:], in_=powers_of[mid][:], axis=AXIS.X, op=ALU.add
-                )
+                summed = powers_of[mid]
+                total = work.tile([P, summed.shape[1], summed.shape[2]], F32)
+                nc.vector.tensor_reduce(out=total[:], in_=summed[:], axis=AXIS.X, op=ALU.add)
             if new is not None:
-                powers = work.tile([P, z.shape[1], GROUP], F32)
+                powers = work.tile([P, z.shape[1], z.shape[2], GROUP], F32)
                 nc.vector.tensor_tensor(
                     out=powers[:], in0=z, in1=over_group(top[:]), op=ALU.subtract
                 )
                 nc.scalar.activation(out=powers[:], in_=powers[:], func=ACT.Exp)
                 powers_of[new] = powers
             if mid is not None:
-                inverse = work.tile([P, powers_of[mid].shape[1]], F32)
+                inverse = work.tile([P, summed.shape[1], summed.shape[2]], F32)
                 nc.vector.reciprocal(out=inverse[:], in_=total[:])
                 inverse_of[mid] = inverse
 
         bias = keep.tile([P, CHUNKS, EXPERTS], F32)
-        mix_rows = keep.tile([P, ROW_TILES, AGENTS, EXPERTS], F32)
-        block_shape = [P, BLOCKS, ROWS_PER_BLOCK, AGENTS]
-        mix_blocks = keep.tile(block_shape, F32)
 
         def transpose_bias():
             b3_ps = psum.tile([P, CHUNKS, P], F32, tag="out")
@@ -145,45 +154,44 @@ def tile_softmoedynamics_pb_e_kernel(tc, h2, logits, W3_words, W3_scales, b3, ou
                 nc.tensor.transpose(b3_ps[:, c, :], b3_wide[:, c * P : (c + 1) * P], identity[:])
             nc.vector.tensor_copy(out=bias[:], in_=b3_ps[:, :, 0:EXPERTS])
 
-        mix_ie = keep.tile([P, ROWS_PER_BLOCK, EXPERTS], F32)
-        same_row = keep.tile([P, ROWS_PER_BLOCK], F32)
+        mix_rows = keep.tile([P, 1, AGENTS * EXPERTS], F32)
+        z_of["mix rows"] = logit_rows[:]
+        y_of["mix rows"] = mix_rows[:]
+        mix_ie = keep.tile([P, 1, ROWS_PER_BLOCK * EXPERTS], F32)
+        z_of["mix blocks"] = logit_blocks[:]
+        y_of["mix blocks"] = mix_ie[:]
+        block_shape = [P, BLOCKS, ROWS_PER_BLOCK, AGENTS]
+        mix_blocks = keep.tile(block_shape, F32)
 
-        def mixing_softmaxes():
-            z_of["mix rows"] = logit_rows[:].rearrange("b t c -> b (t c)")
-            y_of["mix rows"] = mix_rows[:].rearrange("b t n e -> b (t n e)")
-            z_of["mix blocks"] = logit_blocks[:].rearrange("p i e -> p (i e)")
-            y_of["mix blocks"] = mix_ie[:].rearrange("p i e -> p (i e)")
-            softmax_step(new="mix rows")
-            softmax_step(new="mix blocks", mid="mix rows")
+        def build_mix_blocks():
+            same_row = keep.tile([P, ROWS_PER_BLOCK], F32)
             nc.vector.tensor_reduce(
                 out=same_row[:],
                 in_=identity[:].rearrange("p (e i) -> p i e", i=ROWS_PER_BLOCK),
                 axis=AXIS.X,
                 op=ALU.add,
             )
-            softmax_step(mid="mix blocks", old="mix rows")
-            softmax_step(old="mix blocks")
-
-        def build_mix_blocks():
             mix_ei = keep.tile([P, EXPERTS, ROWS_PER_BLOCK], F32)
-            nc.vector.tensor_copy(out=mix_ei[:], in_=mix_ie[:].rearrange("p i e -> p e i"))
-            mix_ps = psum.tile([P, BLOCKS, AGENTS], F32, tag="out")
+            nc.vector.tensor_copy(
+                out=mix_ei[:], in_=mix_ie[:, 0, :].rearrange("p (i e) -> p e i", e=EXPERTS)
+            )
+            mix_ps = psum.tile([P, AGENTS, BLOCKS], F32, tag="out")
             nc.tensor.transpose(
-                mix_ps[:].rearrange("p j n -> p (j n)"),
+                mix_ps[:].rearrange("p n j -> p (n j)"),
                 mix_ei[:].rearrange("p e i -> p (e i)"),
                 identity[:],
             )
             nc.vector.tensor_tensor(
                 out=mix_blocks[:],
-                in0=mix_ps[:].unsqueeze(2).to_broadcast(block_shape),
+                in0=mix_ps[:].rearrange("p n j -> p j n").unsqueeze(2).to_broadcast(block_shape),
                 in1=same_row[:].unsqueeze(1).unsqueeze(3).to_broadcast(block_shape),
                 op=ALU.mult,
             )
 
         h_words = keep.tile([P, EXPERTS, PASSES, BATCH], U32, align_bytes=64)
         h_scales = keep.tile([P, EXPERTS, PASSES, BATCH], U8, align_bytes=64)
-        zT_blocks = keep.tile([P, TENSOR_CHUNKS, BLOCKS, EXPERTS, ROWS_PER_BLOCK], F32)
-        zT_rows = keep.tile([P, EXPERTS, BATCH], F32)
+        zT_blocks = keep.tile([P, CHUNKS, BLOCKS, EXPERTS, ROWS_PER_BLOCK], F32)
+        zT_rows = keep.tile([P, CHUNKS, EXPERTS, P], F32)
 
         def quantise_expert(e):
             grouped = work.tile([P, PASSES, BATCH, PACK], BF16, align_bytes=64)
@@ -224,83 +232,87 @@ def tile_softmoedynamics_pb_e_kernel(tc, h2, logits, W3_words, W3_scales, b3, ou
                         start=(g == 0),
                         stop=(g == PASSES - 1),
                     )
-                if c < TENSOR_CHUNKS:
+                tiles = len([t for t in range(ROW_TILES) if tensor_width(c, t) > 0])
+                nc.scalar.activation(
+                    out=zT_blocks[:, c, 0 : tiles * BLOCKS_PER_TILE, e, :],
+                    in_=zT_ps[:, 0 : tiles * P].rearrange("p (j i) -> p j i", i=ROWS_PER_BLOCK),
+                    func=ACT.Identity,
+                    bias=bias[:, c, e : e + 1],
+                    scale=1.0,
+                )
+                if c >= VECTOR_CHUNK:
                     nc.scalar.activation(
-                        out=zT_blocks[:, c, :, e, :],
-                        in_=zT_ps[:].rearrange("p (i j) -> p j i", j=BLOCKS),
-                        func=ACT.Identity,
-                        bias=bias[:, c, e : e + 1],
-                        scale=1.0,
-                    )
-                else:
-                    nc.scalar.activation(
-                        out=zT_rows[:, e, :],
-                        in_=zT_ps[:],
+                        out=zT_rows[:, c, e, :],
+                        in_=zT_ps[:, BATCH - P : BATCH],
                         func=ACT.Identity,
                         bias=bias[:, c, e : e + 1],
                         scale=1.0,
                     )
 
-        y_rows = keep.tile([P, EXPERTS, ROW_TILES, P], F32)
-        out_rows = keep.tile([P, ROW_TILES, AGENTS, P], F32)
-        experts_per_round = BANK // (ROW_TILES * P)
+        row_chunks = CHUNKS - VECTOR_CHUNK
+        skipped = VECTOR_FIRST - VECTOR_CHUNK * P
+        experts_per_round = BANK // (row_chunks * P)
         row_rounds = EXPERTS // experts_per_round
+        y_rows = keep.tile([P, EXPERTS, VECTOR_COLS], F32)
+        out_rows = keep.tile([P, AGENTS, VECTOR_COLS], F32)
 
         def spread_rows(r):
             first = r * experts_per_round
-            z_ps = psum.tile([P, experts_per_round, ROW_TILES, P], F32, tag="in")
+            z_ps = psum.tile([P, experts_per_round, row_chunks, P], F32, tag="in")
             for e in range(first, first + experts_per_round):
-                for t in range(ROW_TILES):
+                for c in range(VECTOR_CHUNK, CHUNKS):
                     nc.tensor.transpose(
-                        z_ps[:, e - first, t, :], zT_rows[:, e, t * P : (t + 1) * P], identity[:]
+                        z_ps[:, e - first, c - VECTOR_CHUNK, :], zT_rows[:, c, e, :], identity[:]
                     )
-            z_of[("rows", r)] = z_ps[:].rearrange("p e t l -> p (e t l)")
-            y_of[("rows", r)] = y_rows[:, first : first + experts_per_round, :, :].rearrange(
-                "p e t l -> p (e t l)"
-            )
+            z_of[("rows", r)] = z_ps[:].rearrange("p e c l -> p e (c l)")[:, :, skipped:]
+            y_of[("rows", r)] = y_rows[:, first : first + experts_per_round, :]
 
         def weigh_expert(e):
-            for t in range(ROW_TILES):
-                for n in range(AGENTS):
-                    if e == 0:
-                        nc.vector.tensor_scalar_mul(
-                            out=out_rows[:, t, n, :],
-                            in0=y_rows[:, e, t, :],
-                            scalar1=mix_rows[:, t, n, e : e + 1],
-                        )
-                    else:
-                        nc.vector.scalar_tensor_tensor(
-                            out=out_rows[:, t, n, :],
-                            in0=y_rows[:, e, t, :],
-                            scalar=mix_rows[:, t, n, e : e + 1],
-                            in1=out_rows[:, t, n, :],
-                            op0=ALU.mult,
-                            op1=ALU.add,
-                        )
+            for n in range(AGENTS):
+                weight = mix_rows[:, 0, n * EXPERTS + e : n * EXPERTS + e + 1]
+                if e == 0:
+                    nc.vector.tensor_scalar_mul(
+                        out=out_rows[:, n, :], in0=y_rows[:, e, :], scalar1=weight
+                    )
+                else:
+                    nc.vector.scalar_tensor_tensor(
+                        out=out_rows[:, n, :],
+                        in0=y_rows[:, e, :],
+                        scalar=weight,
+                        in1=out_rows[:, n, :],
+                        op0=ALU.mult,
+                        op1=ALU.add,
+                    )
 
-        out_by_block = out.rearrange("(i j) n l -> j i n l", j=BLOCKS)
-        blocks_per_round = BANK // TENSOR_COLS
-        block_rounds = BLOCKS // blocks_per_round
+        out_flat = out.rearrange("b n l -> (b n) l")
+        blocks_per_round = BANK // P
+        block_rounds = [
+            (c, first)
+            for c in range(CHUNKS)
+            for first in range(0, BLOCKS, blocks_per_round)
+            if tensor_width(c, first // BLOCKS_PER_TILE) > 0
+        ]
         y_blocks_of = {}
 
         def spread_blocks(r):
-            first = r * blocks_per_round
-            z_ps = psum.tile([P, blocks_per_round, TENSOR_CHUNKS, P], F32, tag="in")
+            c, first = block_rounds[r]
+            width = tensor_width(c, first // BLOCKS_PER_TILE)
+            z_ps = psum.tile([P, blocks_per_round, P], F32, tag="in")
             for j in range(first, first + blocks_per_round):
-                for c in range(TENSOR_CHUNKS):
-                    nc.tensor.transpose(
-                        z_ps[:, j - first, c, :],
-                        zT_blocks[:, c, j, :, :].rearrange("p e i -> p (e i)"),
-                        identity[:],
-                    )
-            y_blocks = work.tile([P, blocks_per_round, TENSOR_COLS], F32)
-            z_of[("blocks", r)] = z_ps[:].rearrange("p j c l -> p (j c l)")
-            y_of[("blocks", r)] = y_blocks[:].rearrange("p j l -> p (j l)")
+                nc.tensor.transpose(
+                    z_ps[:, j - first, :],
+                    zT_blocks[:, c, j, :, :].rearrange("p e i -> p (e i)"),
+                    identity[:],
+                )
+            y_blocks = work.tile([P, blocks_per_round, width], F32)
+            z_of[("blocks", r)] = z_ps[:, :, 0:width]
+            y_of[("blocks", r)] = y_blocks[:]
             y_blocks_of[r] = y_blocks
 
         def combine_blocks(r):
-            first = r * blocks_per_round
-            sum_ps = psum.tile([P, blocks_per_round, TENSOR_COLS], F32, tag="out")
+            c, first = block_rounds[r]
+            width = tensor_width(c, first // BLOCKS_PER_TILE)
+            sum_ps = psum.tile([P, blocks_per_round, width], F32, tag="out")
             for j in range(first, first + blocks_per_round):
                 nc.tensor.matmul(
                     out=sum_ps[:, j - first, :],
@@ -309,50 +321,50 @@ def tile_softmoedynamics_pb_e_kernel(tc, h2, logits, W3_words, W3_scales, b3, ou
                     start=True,
                     stop=True,
                 )
-            out_blocks = work.tile([P, blocks_per_round, TENSOR_COLS], F32)
+            out_blocks = work.tile([P, blocks_per_round, width], F32)
             nc.scalar.copy(out=out_blocks[:], in_=sum_ps[:])
-            for j in range(first, first + blocks_per_round):
-                nc.sync.dma_start(
-                    out=out_by_block[j, :, :, 0:TENSOR_COLS], in_=out_blocks[:, j - first, :]
-                )
+            nc.sync.dma_start(
+                out=out_flat[
+                    first * P : (first + blocks_per_round) * P, c * P : c * P + width
+                ].rearrange("(j m) l -> m j l", m=P),
+                in_=out_blocks[:],
+            )
 
-        rounds = [("rows", r) for r in range(row_rounds)] + [
-            ("blocks", r) for r in range(block_rounds)
-        ]
+        rounds = (
+            ["mix rows"]
+            + [("rows", r) for r in range(row_rounds)]
+            + ["mix blocks"]
+            + [("blocks", r) for r in range(len(block_rounds))]
+        )
 
         def round_at(k):
             return rounds[k] if 0 <= k < len(rounds) else None
 
-        def round_step(k):
-            softmax_step(new=round_at(k), mid=round_at(k - 1), old=round_at(k - 2))
+        def chain_step(k):
+            new = round_at(k)
+            old = round_at(k - 2)
+            if new is not None and new[0] == "rows":
+                spread_rows(new[1])
+            if new is not None and new[0] == "blocks":
+                spread_blocks(new[1])
+            softmax_step(new, round_at(k - 1), old)
+            if old == "mix blocks":
+                build_mix_blocks()
+            if old is not None and old[0] == "blocks":
+                combine_blocks(old[1])
+            if k % 2 == 1 and 0 <= (k - 3) // 2 < EXPERTS:
+                weigh_expert((k - 3) // 2)
 
         quantise_expert(0)
         transpose_bias()
         quantise_expert(1)
-        mixing_softmaxes()
-        for e in range(experts_per_round):
-            quantise_expert(e + 2)
-            expert_layer(e)
-        build_mix_blocks()
-        for e in range(experts_per_round, EXPERTS):
+        chain_step(0)
+        for e in range(EXPERTS):
             if e + 2 < EXPERTS:
                 quantise_expert(e + 2)
             expert_layer(e)
-            if e % experts_per_round == 0:
-                spread_rows(e // experts_per_round - 1)
-                round_step(e // experts_per_round - 1)
-        spread_rows(row_rounds - 1)
-        round_step(row_rounds - 1)
-
-        assert block_rounds == EXPERTS
-        for s in range(block_rounds + 2):
-            if s < block_rounds:
-                spread_blocks(s)
-            round_step(row_rounds + s)
-            if s >= 2:
-                combine_blocks(s - 2)
-                weigh_expert(s - 2)
-        for t in range(ROW_TILES):
-            nc.sync.dma_start(
-                out=out[t * P : (t + 1) * P, :, TENSOR_COLS:COLS], in_=out_rows[:, t, :, :]
-            )
+            if e >= experts_per_round and e % experts_per_round == 0:
+                chain_step(e // experts_per_round)
+        for k in range(row_rounds, len(rounds) + 2):
+            chain_step(k)
+        nc.sync.dma_start(out=out[BATCH - P : BATCH, :, VECTOR_FIRST:COLS], in_=out_rows[:])

@@ -86,7 +86,7 @@ def tile_softmoedynamics_pb_e_kernel(tc, h2, logits, W3_words, W3_scales, b3, ou
                 .rearrange("g r n -> r g n")
                 .bitcast(I32),
             )
-        for e in range(2, EXPERTS):
+        for e in range(2, 4):
             load_expert(e)
         logit_blocks = keep.tile([P, 1, ROWS_PER_BLOCK * EXPERTS], BF16)
         for n in range(AGENTS):
@@ -97,6 +97,8 @@ def tile_softmoedynamics_pb_e_kernel(tc, h2, logits, W3_words, W3_scales, b3, ou
                 in_=logits[:, n, :].rearrange("(j i) e -> j i e", i=ROWS_PER_BLOCK),
             )
 
+        for e in range(4, EXPERTS):
+            load_expert(e)
         warm = keep.tile([P, 1], F32)
         nc.vector.memset(warm[:], 0.0)
         nc.scalar.activation(out=warm[:], in_=warm[:], func=ACT.Exp)
@@ -205,7 +207,8 @@ def tile_softmoedynamics_pb_e_kernel(tc, h2, logits, W3_words, W3_scales, b3, ou
                             pairs[:, g * 2 * P + u : (g + 1) * 2 * P : 2],
                             identity[:],
                         )
-                nc.scalar.copy(
+                copier = nc.scalar.copy if g == 0 else nc.vector.tensor_copy
+                copier(
                     out=grouped[:, g, :, :]
                     .rearrange("p b k -> p (b k)")
                     .bitcast(F32)
@@ -330,41 +333,43 @@ def tile_softmoedynamics_pb_e_kernel(tc, h2, logits, W3_words, W3_scales, b3, ou
                 in_=out_blocks[:],
             )
 
-        rounds = (
-            ["mix rows"]
-            + [("rows", r) for r in range(row_rounds)]
-            + ["mix blocks"]
-            + [("blocks", r) for r in range(len(block_rounds))]
-        )
+        rounds = ["mix rows", "mix blocks"]
+        for r in range(row_rounds):
+            rounds.extend([("rows", r)] + [None] * (experts_per_round - 1))
+        first_rows = rounds.index(("rows", 0))
+        first_blocks = len(rounds) - (experts_per_round - 1)
+        rounds = rounds[0:first_blocks] + [("blocks", r) for r in range(len(block_rounds))]
 
         def round_at(k):
             return rounds[k] if 0 <= k < len(rounds) else None
 
         def chain_step(k):
-            new = round_at(k)
+            ahead = round_at(k + 1)
             old = round_at(k - 2)
+            if ahead is not None and ahead[0] == "blocks":
+                spread_blocks(ahead[1])
+            new = round_at(k)
             if new is not None and new[0] == "rows":
                 spread_rows(new[1])
-            if new is not None and new[0] == "blocks":
-                spread_blocks(new[1])
             softmax_step(new, round_at(k - 1), old)
             if old == "mix blocks":
                 build_mix_blocks()
             if old is not None and old[0] == "blocks":
                 combine_blocks(old[1])
-            if k % 2 == 1 and 0 <= (k - 3) // 2 < EXPERTS:
-                weigh_expert((k - 3) // 2)
+            if 0 <= k - first_rows - 2 < EXPERTS - 1:
+                weigh_expert(k - first_rows - 2)
 
+        assert first_rows == experts_per_round
         quantise_expert(0)
         transpose_bias()
-        quantise_expert(1)
-        chain_step(0)
         for e in range(EXPERTS):
-            if e + 2 < EXPERTS:
-                quantise_expert(e + 2)
+            if e + 1 < EXPERTS:
+                quantise_expert(e + 1)
             expert_layer(e)
-            if e >= experts_per_round and e % experts_per_round == 0:
-                chain_step(e // experts_per_round)
-        for k in range(row_rounds, len(rounds) + 2):
+            chain_step(e)
+        for k in range(EXPERTS, len(rounds) + 1):
             chain_step(k)
+        softmax_step(None, None, rounds[-1])
+        weigh_expert(EXPERTS - 1)
         nc.sync.dma_start(out=out[BATCH - P : BATCH, :, VECTOR_FIRST:COLS], in_=out_rows[:])
+        combine_blocks(len(block_rounds) - 1)

@@ -78,7 +78,6 @@ def tile_softmoedynamics_pb_e_kernel(tc, h2, logits, W3_words, W3_scales, b3, ou
             )
 
         load_expert(0)
-        load_expert(1)
         for quadrant in range(4):
             nc.sync.dma_start(
                 out=w_scales[32 * quadrant : 32 * quadrant + 4, :, :].bitcast(I32),
@@ -86,7 +85,7 @@ def tile_softmoedynamics_pb_e_kernel(tc, h2, logits, W3_words, W3_scales, b3, ou
                 .rearrange("g r n -> r g n")
                 .bitcast(I32),
             )
-        for e in range(2, 4):
+        for e in range(1, 4):
             load_expert(e)
         logit_blocks = keep.tile([P, 1, ROWS_PER_BLOCK * EXPERTS], BF16)
         for n in range(AGENTS):
@@ -207,7 +206,7 @@ def tile_softmoedynamics_pb_e_kernel(tc, h2, logits, W3_words, W3_scales, b3, ou
                             pairs[:, g * 2 * P + u : (g + 1) * 2 * P : 2],
                             identity[:],
                         )
-                copier = nc.scalar.copy if g == 0 else nc.vector.tensor_copy
+                copier = nc.vector.tensor_copy if g == 0 else nc.scalar.copy
                 copier(
                     out=grouped[:, g, :, :]
                     .rearrange("p b k -> p (b k)")
@@ -333,10 +332,11 @@ def tile_softmoedynamics_pb_e_kernel(tc, h2, logits, W3_words, W3_scales, b3, ou
                 in_=out_blocks[:],
             )
 
-        rounds = ["mix rows", "mix blocks"]
+        rounds = ["mix rows", None]
         for r in range(row_rounds):
             rounds.extend([("rows", r)] + [None] * (experts_per_round - 1))
         first_rows = rounds.index(("rows", 0))
+        rounds[first_rows + 1] = "mix blocks"
         first_blocks = len(rounds) - (experts_per_round - 1)
         rounds = rounds[0:first_blocks] + [("blocks", r) for r in range(len(block_rounds))]
 

@@ -36,6 +36,7 @@ ROWS_PER_BLOCK = P // EXPERTS
 BLOCKS = BATCH // ROWS_PER_BLOCK
 BLOCKS_PER_TILE = P // ROWS_PER_BLOCK
 VECTOR_COLS = 160
+VECTOR_COPIES = 0
 assert 10 * (2 * P * AGENTS * (BATCH * COLS - P * VECTOR_COLS)) <= MX_FLOPS
 VECTOR_FIRST = COLS - VECTOR_COLS
 VECTOR_CHUNK = VECTOR_FIRST // P
@@ -110,7 +111,9 @@ def tile_softmoedynamics_pb_e_kernel(tc, h2, logits, W3_words, W3_scales, b3, ou
 
         z_of = {}
         y_of = {}
+        top_of = {}
         powers_of = {}
+        total_of = {}
         inverse_of = {}
 
         def by_group(ap):
@@ -119,33 +122,62 @@ def tile_softmoedynamics_pb_e_kernel(tc, h2, logits, W3_words, W3_scales, b3, ou
         def over_group(ap):
             return ap.unsqueeze(3).to_broadcast([P, ap.shape[1], ap.shape[2], GROUP])
 
-        def softmax_step(new, mid, old):
-            if new is not None:
-                z = by_group(z_of[new])
-                top = work.tile([P, z.shape[1], z.shape[2]], F32)
-                nc.vector.tensor_reduce(out=top[:], in_=z, axis=AXIS.X, op=ALU.max)
-            if old is not None:
+        def find_tops(name, which):
+            views = z_of[name]
+            if 0 in which:
+                top = work.tile([P, len(views), views[0].shape[1], views[0].shape[2] // GROUP], F32)
+                top_of[name] = top
+            for v in which:
+                nc.vector.tensor_reduce(
+                    out=top_of[name][:, v, :, :], in_=by_group(views[v]), axis=AXIS.X, op=ALU.max
+                )
+
+        def raise_powers(name):
+            views = z_of[name]
+            top = top_of[name]
+            shape = [P, len(views), views[0].shape[1], views[0].shape[2] // GROUP, GROUP]
+            powers = work.tile(shape, F32)
+            for v in range(len(views)):
                 nc.vector.tensor_tensor(
-                    out=by_group(y_of[old]),
-                    in0=powers_of[old][:],
-                    in1=over_group(inverse_of[old][:]),
+                    out=powers[:, v, :, :, :],
+                    in0=by_group(views[v]),
+                    in1=over_group(top[:, v, :, :]),
+                    op=ALU.subtract,
+                )
+                nc.scalar.activation(
+                    out=powers[:, v, :, :, :], in_=powers[:, v, :, :, :], func=ACT.Exp
+                )
+            powers_of[name] = powers
+
+        def sum_powers(name):
+            powers = powers_of[name]
+            total = work.tile([P, powers.shape[1], powers.shape[2], powers.shape[3]], F32)
+            nc.vector.tensor_reduce(
+                out=total[:].rearrange("p v a g -> p (v a g)"),
+                in_=powers[:].rearrange("p v a g i -> p (v a g) i"),
+                axis=AXIS.X,
+                op=ALU.add,
+            )
+            total_of[name] = total
+
+        def invert_sums(name):
+            total = total_of[name]
+            inverse = work.tile([P, total.shape[1], total.shape[2], total.shape[3]], F32)
+            nc.vector.reciprocal(
+                out=inverse[:].rearrange("p v a g -> p (v a g)"),
+                in_=total[:].rearrange("p v a g -> p (v a g)"),
+            )
+            inverse_of[name] = inverse
+
+        def scale_powers(name, engine):
+            places = y_of[name]
+            for v in range(len(places)):
+                engine.tensor_tensor(
+                    out=by_group(places[v]),
+                    in0=powers_of[name][:, v, :, :, :],
+                    in1=over_group(inverse_of[name][:, v, :, :]),
                     op=ALU.mult,
                 )
-            if mid is not None:
-                summed = powers_of[mid]
-                total = work.tile([P, summed.shape[1], summed.shape[2]], F32)
-                nc.vector.tensor_reduce(out=total[:], in_=summed[:], axis=AXIS.X, op=ALU.add)
-            if new is not None:
-                powers = work.tile([P, z.shape[1], z.shape[2], GROUP], F32)
-                nc.vector.tensor_tensor(
-                    out=powers[:], in0=z, in1=over_group(top[:]), op=ALU.subtract
-                )
-                nc.scalar.activation(out=powers[:], in_=powers[:], func=ACT.Exp)
-                powers_of[new] = powers
-            if mid is not None:
-                inverse = work.tile([P, summed.shape[1], summed.shape[2]], F32)
-                nc.vector.reciprocal(out=inverse[:], in_=total[:])
-                inverse_of[mid] = inverse
 
         bias = keep.tile([P, CHUNKS, EXPERTS], F32)
 
@@ -156,11 +188,11 @@ def tile_softmoedynamics_pb_e_kernel(tc, h2, logits, W3_words, W3_scales, b3, ou
             nc.vector.tensor_copy(out=bias[:], in_=b3_ps[:, :, 0:EXPERTS])
 
         mix_rows = keep.tile([P, 1, AGENTS * EXPERTS], F32)
-        z_of["mix rows"] = logit_rows[:]
-        y_of["mix rows"] = mix_rows[:]
+        z_of["mix rows"] = [logit_rows[:]]
+        y_of["mix rows"] = [mix_rows[:]]
         mix_ie = keep.tile([P, 1, ROWS_PER_BLOCK * EXPERTS], F32)
-        z_of["mix blocks"] = logit_blocks[:]
-        y_of["mix blocks"] = mix_ie[:]
+        z_of["mix blocks"] = [logit_blocks[:]]
+        y_of["mix blocks"] = [mix_ie[:]]
         block_shape = [P, BLOCKS, ROWS_PER_BLOCK, AGENTS]
         mix_blocks = keep.tile(block_shape, F32)
 
@@ -206,7 +238,7 @@ def tile_softmoedynamics_pb_e_kernel(tc, h2, logits, W3_words, W3_scales, b3, ou
                             pairs[:, g * 2 * P + u : (g + 1) * 2 * P : 2],
                             identity[:],
                         )
-                copier = nc.vector.tensor_copy if g == 0 else nc.scalar.copy
+                copier = nc.vector.tensor_copy if g < VECTOR_COPIES else nc.scalar.copy
                 copier(
                     out=grouped[:, g, :, :]
                     .rearrange("p b k -> p (b k)")
@@ -266,15 +298,15 @@ def tile_softmoedynamics_pb_e_kernel(tc, h2, logits, W3_words, W3_scales, b3, ou
                     nc.tensor.transpose(
                         z_ps[:, e - first, c - VECTOR_CHUNK, :], zT_rows[:, c, e, :], identity[:]
                     )
-            z_of[("rows", r)] = z_ps[:].rearrange("p e c l -> p e (c l)")[:, :, skipped:]
-            y_of[("rows", r)] = y_rows[:, first : first + experts_per_round, :]
+            z_of[("rows", r)] = [z_ps[:].rearrange("p e c l -> p e (c l)")[:, :, skipped:]]
+            y_of[("rows", r)] = [y_rows[:, first : first + experts_per_round, :]]
 
         def weigh_expert(e):
             for n in range(AGENTS):
                 weight = mix_rows[:, 0, n * EXPERTS + e : n * EXPERTS + e + 1]
                 if e == 0:
-                    nc.vector.tensor_scalar_mul(
-                        out=out_rows[:, n, :], in0=y_rows[:, e, :], scalar1=weight
+                    nc.scalar.activation(
+                        out=out_rows[:, n, :], in_=y_rows[:, e, :], func=ACT.Identity, scale=weight
                     )
                 else:
                     nc.vector.scalar_tensor_tensor(
@@ -288,76 +320,106 @@ def tile_softmoedynamics_pb_e_kernel(tc, h2, logits, W3_words, W3_scales, b3, ou
 
         out_flat = out.rearrange("b n l -> (b n) l")
         blocks_per_round = BANK // P
-        block_rounds = [
-            (c, first)
-            for c in range(CHUNKS)
-            for first in range(0, BLOCKS, blocks_per_round)
-            if tensor_width(c, first // BLOCKS_PER_TILE) > 0
+        rounds_per_item = BLOCKS_PER_TILE // blocks_per_round
+        block_items = [
+            (c, t) for c in range(CHUNKS) for t in range(ROW_TILES) if tensor_width(c, t) > 0
         ]
-        y_blocks_of = {}
+        block_items = sorted(block_items, key=lambda ct: -tensor_width(ct[0], ct[1]))
 
-        def spread_blocks(r):
-            c, first = block_rounds[r]
-            width = tensor_width(c, first // BLOCKS_PER_TILE)
-            z_ps = psum.tile([P, blocks_per_round, P], F32, tag="in")
-            for j in range(first, first + blocks_per_round):
-                nc.tensor.transpose(
-                    z_ps[:, j - first, :],
-                    zT_blocks[:, c, j, :, :].rearrange("p e i -> p (e i)"),
-                    identity[:],
+        def spread_blocks(q):
+            c, t = block_items[q]
+            width = tensor_width(c, t)
+            views = []
+            for v in range(rounds_per_item):
+                first = t * BLOCKS_PER_TILE + v * blocks_per_round
+                z_ps = psum.tile([P, blocks_per_round, P], F32, tag="in")
+                for j in range(first, first + blocks_per_round):
+                    nc.tensor.transpose(
+                        z_ps[:, j - first, :],
+                        zT_blocks[:, c, j, :, :].rearrange("p e i -> p (e i)"),
+                        identity[:],
+                    )
+                views.append(z_ps[:, :, 0:width])
+            z_of[("blocks", q)] = views
+
+        def place_blocks(q):
+            c, t = block_items[q]
+            y_blocks = work.tile([P, rounds_per_item, blocks_per_round, tensor_width(c, t)], F32)
+            y_of[("blocks", q)] = [y_blocks[:, v, :, :] for v in range(rounds_per_item)]
+
+        def combine_blocks(q):
+            c, t = block_items[q]
+            width = tensor_width(c, t)
+            for v in range(rounds_per_item):
+                first = t * BLOCKS_PER_TILE + v * blocks_per_round
+                sum_ps = psum.tile([P, blocks_per_round, width], F32, tag="out")
+                for j in range(first, first + blocks_per_round):
+                    nc.tensor.matmul(
+                        out=sum_ps[:, j - first, :],
+                        lhsT=mix_blocks[:, j, :, :].rearrange("p i n -> p (i n)"),
+                        rhs=y_of[("blocks", q)][v][:, j - first, :],
+                        start=True,
+                        stop=True,
+                    )
+                out_blocks = work.tile([P, blocks_per_round, width], F32)
+                nc.scalar.copy(out=out_blocks[:], in_=sum_ps[:])
+                nc.sync.dma_start(
+                    out=out_flat[
+                        first * P : (first + blocks_per_round) * P, c * P : c * P + width
+                    ].rearrange("(j m) l -> m j l", m=P),
+                    in_=out_blocks[:],
                 )
-            y_blocks = work.tile([P, blocks_per_round, width], F32)
-            z_of[("blocks", r)] = z_ps[:, :, 0:width]
-            y_of[("blocks", r)] = y_blocks[:]
-            y_blocks_of[r] = y_blocks
 
-        def combine_blocks(r):
-            c, first = block_rounds[r]
-            width = tensor_width(c, first // BLOCKS_PER_TILE)
-            sum_ps = psum.tile([P, blocks_per_round, width], F32, tag="out")
-            for j in range(first, first + blocks_per_round):
-                nc.tensor.matmul(
-                    out=sum_ps[:, j - first, :],
-                    lhsT=mix_blocks[:, j, :, :].rearrange("p i n -> p (i n)"),
-                    rhs=y_blocks_of[r][:, j - first, :],
-                    start=True,
-                    stop=True,
-                )
-            out_blocks = work.tile([P, blocks_per_round, width], F32)
-            nc.scalar.copy(out=out_blocks[:], in_=sum_ps[:])
-            nc.sync.dma_start(
-                out=out_flat[
-                    first * P : (first + blocks_per_round) * P, c * P : c * P + width
-                ].rearrange("(j m) l -> m j l", m=P),
-                in_=out_blocks[:],
-            )
-
-        rounds = ["mix rows", None]
+        chain = ["mix rows", None]
         for r in range(row_rounds):
-            rounds.extend([("rows", r)] + [None] * (experts_per_round - 1))
-        first_rows = rounds.index(("rows", 0))
-        rounds[first_rows + 1] = "mix blocks"
-        first_blocks = len(rounds) - (experts_per_round - 1)
-        rounds = rounds[0:first_blocks] + [("blocks", r) for r in range(len(block_rounds))]
+            chain.extend([("rows", r)] + [None] * (experts_per_round - 1))
+        first_rows = chain.index(("rows", 0))
+        chain[first_rows + 1] = "mix blocks"
+        first_blocks = len(chain) - (experts_per_round - 1)
+        chain = chain[0:first_blocks] + [("blocks", q) for q in range(len(block_items))]
 
-        def round_at(k):
-            return rounds[k] if 0 <= k < len(rounds) else None
+        def item_at(k):
+            return chain[k] if 0 <= k < len(chain) else None
+
+        def is_blocks(name):
+            return name is not None and name[0] == "blocks"
 
         def chain_step(k):
-            ahead = round_at(k + 1)
-            old = round_at(k - 2)
-            if ahead is not None and ahead[0] == "blocks":
-                spread_blocks(ahead[1])
-            new = round_at(k)
+            ahead, new, mid, old = [item_at(k + 1 - d) for d in range(4)]
+            weighed = k - first_rows - 1
             if new is not None and new[0] == "rows":
                 spread_rows(new[1])
-            softmax_step(new, round_at(k - 1), old)
-            if old == "mix blocks":
-                build_mix_blocks()
-            if old is not None and old[0] == "blocks":
+            if is_blocks(ahead):
+                spread_blocks(ahead[1])
+            if is_blocks(old):
                 combine_blocks(old[1])
-            if 0 <= k - first_rows - 2 < EXPERTS - 1:
-                weigh_expert(k - first_rows - 2)
+            if new is not None:
+                find_tops(new, [0])
+            if mid is not None:
+                sum_powers(mid)
+            if new is not None:
+                find_tops(new, range(1, len(z_of[new])))
+            if 0 <= weighed < EXPERTS and weighed % experts_per_round > 0:
+                weigh_expert(weighed)
+            if weighed == EXPERTS - 1:
+                nc.sync.dma_start(
+                    out=out[BATCH - P : BATCH, :, VECTOR_FIRST:COLS], in_=out_rows[:]
+                )
+            if mid is not None:
+                invert_sums(mid)
+            by_gpsimd = is_blocks(mid) and mid != chain[-1]
+            if is_blocks(mid):
+                place_blocks(mid[1])
+            if by_gpsimd:
+                scale_powers(mid, nc.gpsimd)
+            if new is not None:
+                raise_powers(new)
+            if mid is not None and not by_gpsimd:
+                scale_powers(mid, nc.vector)
+            if mid == "mix blocks":
+                build_mix_blocks()
+            if 0 <= weighed < EXPERTS and weighed % experts_per_round == 0:
+                weigh_expert(weighed)
 
         assert first_rows == experts_per_round
         quantise_expert(0)
@@ -367,9 +429,5 @@ def tile_softmoedynamics_pb_e_kernel(tc, h2, logits, W3_words, W3_scales, b3, ou
                 quantise_expert(e + 1)
             expert_layer(e)
             chain_step(e)
-        for k in range(EXPERTS, len(rounds) + 1):
+        for k in range(EXPERTS, len(chain) + 2):
             chain_step(k)
-        softmax_step(None, None, rounds[-1])
-        weigh_expert(EXPERTS - 1)
-        nc.sync.dma_start(out=out[BATCH - P : BATCH, :, VECTOR_FIRST:COLS], in_=out_rows[:])
-        combine_blocks(len(block_rounds) - 1)

@@ -36,7 +36,6 @@ ROWS_PER_BLOCK = P // EXPERTS
 BLOCKS = BATCH // ROWS_PER_BLOCK
 BLOCKS_PER_TILE = P // ROWS_PER_BLOCK
 VECTOR_COLS = 160
-VECTOR_COPIES = 0
 assert 10 * (2 * P * AGENTS * (BATCH * COLS - P * VECTOR_COLS)) <= MX_FLOPS
 VECTOR_FIRST = COLS - VECTOR_COLS
 VECTOR_CHUNK = VECTOR_FIRST // P
@@ -45,6 +44,13 @@ VECTOR_CHUNK = VECTOR_FIRST // P
 def tensor_width(c, t):
     last = COLS if t < ROW_TILES - 1 else VECTOR_FIRST
     return max(0, min(P, last - c * P))
+
+
+LAST = ROW_TILES - 1
+LOGITS_AFTER = 3
+MIX_AT = 4
+TURN_FIRST = 0
+VECTOR_COPIES = []
 
 
 def tile_softmoedynamics_pb_e_kernel(tc, h2, logits, W3_words, W3_scales, b3, out):
@@ -68,37 +74,37 @@ def tile_softmoedynamics_pb_e_kernel(tc, h2, logits, W3_words, W3_scales, b3, ou
         w_scales = keep.tile([P, EXPERTS * PASSES, COLS], U8, align_bytes=64)
         nc.vector.memset(w_scales[:].bitcast(I32), 0)
 
-        def load_expert(e):
+        def load_rows(e, t):
+            nc.sync.dma_start(out=h2_rows[:, e, t, :], in_=h2[t * P : (t + 1) * P, e, :])
+
+        def load_weights(e):
             passes = slice(e * PASSES, (e + 1) * PASSES)
-            nc.sync.dma_start(
-                out=h2_rows[:, e, :, :], in_=h2[:, e, :].rearrange("(t b) k -> b t k", b=P)
-            )
             nc.sync.dma_start(
                 out=w_words[:, passes, :].bitcast(I32),
                 in_=W3_words[passes].rearrange("g p n t -> p g (n t)").bitcast(I32),
             )
 
-        load_expert(0)
-        for quadrant in range(4):
-            nc.sync.dma_start(
-                out=w_scales[32 * quadrant : 32 * quadrant + 4, :, :].bitcast(I32),
-                in_=W3_scales[:, 4 * quadrant : 4 * quadrant + 4, :]
-                .rearrange("g r n -> r g n")
-                .bitcast(I32),
-            )
-        for e in range(1, 4):
-            load_expert(e)
         logit_blocks = keep.tile([P, 1, ROWS_PER_BLOCK * EXPERTS], BF16)
-        for n in range(AGENTS):
-            nc.sync.dma_start(
-                out=logit_blocks[n * BLOCKS : (n + 1) * BLOCKS, 0, :].rearrange(
-                    "j (i e) -> j i e", e=EXPERTS
-                ),
-                in_=logits[:, n, :].rearrange("(j i) e -> j i e", i=ROWS_PER_BLOCK),
-            )
-
-        for e in range(4, EXPERTS):
-            load_expert(e)
+        for e in range(EXPERTS):
+            load_rows(e, LAST)
+            load_weights(e)
+            load_rows(e, 0)
+            if e == 0:
+                for quadrant in range(4):
+                    nc.sync.dma_start(
+                        out=w_scales[32 * quadrant : 32 * quadrant + 4, :, :].bitcast(I32),
+                        in_=W3_scales[:, 4 * quadrant : 4 * quadrant + 4, :]
+                        .rearrange("g r n -> r g n")
+                        .bitcast(I32),
+                    )
+            if e == LOGITS_AFTER:
+                for n in range(AGENTS):
+                    nc.sync.dma_start(
+                        out=logit_blocks[n * BLOCKS : (n + 1) * BLOCKS, 0, :].rearrange(
+                            "j (i e) -> j i e", e=EXPERTS
+                        ),
+                        in_=logits[:, n, :].rearrange("(j i) e -> j i e", i=ROWS_PER_BLOCK),
+                    )
         warm = keep.tile([P, 1], F32)
         nc.vector.memset(warm[:], 0.0)
         nc.scalar.activation(out=warm[:], in_=warm[:], func=ACT.Exp)
@@ -132,22 +138,29 @@ def tile_softmoedynamics_pb_e_kernel(tc, h2, logits, W3_words, W3_scales, b3, ou
                     out=top_of[name][:, v, :, :], in_=by_group(views[v]), axis=AXIS.X, op=ALU.max
                 )
 
-        def raise_powers(name):
+        def raise_powers(name, which=(0,), later=False):
             views = z_of[name]
             top = top_of[name]
             shape = [P, len(views), views[0].shape[1], views[0].shape[2] // GROUP, GROUP]
-            powers = work.tile(shape, F32)
-            for v in range(len(views)):
+            if 0 in which:
+                powers = work.tile(shape, F32)
+                powers_of[name] = powers
+            powers = powers_of[name]
+            for v in which:
                 nc.vector.tensor_tensor(
                     out=powers[:, v, :, :, :],
                     in0=by_group(views[v]),
                     in1=over_group(top[:, v, :, :]),
                     op=ALU.subtract,
                 )
-                nc.scalar.activation(
-                    out=powers[:, v, :, :, :], in_=powers[:, v, :, :, :], func=ACT.Exp
-                )
-            powers_of[name] = powers
+                if not later:
+                    nc.scalar.activation(
+                        out=powers[:, v, :, :, :], in_=powers[:, v, :, :, :], func=ACT.Exp
+                    )
+
+        def exponentiate(name):
+            powers = powers_of[name]
+            nc.scalar.activation(out=powers[:], in_=powers[:], func=ACT.Exp)
 
         def sum_powers(name):
             powers = powers_of[name]
@@ -160,13 +173,25 @@ def tile_softmoedynamics_pb_e_kernel(tc, h2, logits, W3_words, W3_scales, b3, ou
             )
             total_of[name] = total
 
-        def invert_sums(name):
+        minus_one = keep.tile([P, 1], F32)
+        nc.vector.memset(minus_one[:], -1.0)
+
+        def invert_sums(name, by_gpsimd=False):
             total = total_of[name]
             inverse = work.tile([P, total.shape[1], total.shape[2], total.shape[3]], F32)
-            nc.vector.reciprocal(
-                out=inverse[:].rearrange("p v a g -> p (v a g)"),
-                in_=total[:].rearrange("p v a g -> p (v a g)"),
-            )
+            count = total.shape[1] * total.shape[2] * total.shape[3]
+            if by_gpsimd:
+                nc.gpsimd.tensor_tensor(
+                    out=inverse[:].rearrange("p v a g -> p (v a g)"),
+                    in0=total[:].rearrange("p v a g -> p (v a g)"),
+                    in1=minus_one[:].to_broadcast([P, count]),
+                    op=ALU.pow,
+                )
+            else:
+                nc.vector.reciprocal(
+                    out=inverse[:].rearrange("p v a g -> p (v a g)"),
+                    in_=total[:].rearrange("p v a g -> p (v a g)"),
+                )
             inverse_of[name] = inverse
 
         def scale_powers(name, engine):
@@ -195,19 +220,21 @@ def tile_softmoedynamics_pb_e_kernel(tc, h2, logits, W3_words, W3_scales, b3, ou
         y_of["mix blocks"] = [mix_ie[:]]
         block_shape = [P, BLOCKS, ROWS_PER_BLOCK, AGENTS]
         mix_blocks = keep.tile(block_shape, F32)
+        same_row = keep.tile([P, ROWS_PER_BLOCK], F32)
+        mix_ei = keep.tile([P, EXPERTS, ROWS_PER_BLOCK], F32)
 
-        def build_mix_blocks():
-            same_row = keep.tile([P, ROWS_PER_BLOCK], F32)
+        def order_mix():
             nc.vector.tensor_reduce(
                 out=same_row[:],
                 in_=identity[:].rearrange("p (e i) -> p i e", i=ROWS_PER_BLOCK),
                 axis=AXIS.X,
                 op=ALU.add,
             )
-            mix_ei = keep.tile([P, EXPERTS, ROWS_PER_BLOCK], F32)
             nc.vector.tensor_copy(
                 out=mix_ei[:], in_=mix_ie[:, 0, :].rearrange("p (i e) -> p e i", e=EXPERTS)
             )
+
+        def build_mix_blocks():
             mix_ps = psum.tile([P, AGENTS, BLOCKS], F32, tag="out")
             nc.tensor.transpose(
                 mix_ps[:].rearrange("p n j -> p (n j)"),
@@ -221,67 +248,84 @@ def tile_softmoedynamics_pb_e_kernel(tc, h2, logits, W3_words, W3_scales, b3, ou
                 op=ALU.mult,
             )
 
-        h_words = keep.tile([P, EXPERTS, PASSES, BATCH], U32, align_bytes=64)
-        h_scales = keep.tile([P, EXPERTS, PASSES, BATCH], U8, align_bytes=64)
+        h_words = keep.tile([P, EXPERTS, ROW_TILES, PASSES, P], U32, align_bytes=64)
+        h_scales = keep.tile([P, EXPERTS, ROW_TILES, PASSES, P], U8, align_bytes=64)
         zT_blocks = keep.tile([P, CHUNKS, BLOCKS, EXPERTS, ROWS_PER_BLOCK], F32)
-        zT_rows = keep.tile([P, CHUNKS, EXPERTS, P], F32)
 
-        def quantise_expert(e):
-            grouped = work.tile([P, PASSES, BATCH, PACK], BF16, align_bytes=64)
+        pairs_of = {}
+        grouped_of = {}
+
+        def turn(e, t):
+            if e >= EXPERTS:
+                return
+            pairs = h2_rows[:, e, t, :].bitcast(F32)
+            pairs_ps = psum.tile([P, PASSES, 2, P], F32, tag="in")
             for g in range(PASSES):
-                pairs_ps = psum.tile([P, 2, BATCH], F32, tag="in")
-                for t in range(ROW_TILES):
-                    pairs = h2_rows[:, e, t, :].bitcast(F32)
-                    for u in range(2):
-                        nc.tensor.transpose(
-                            pairs_ps[:, u, t * P : (t + 1) * P],
-                            pairs[:, g * 2 * P + u : (g + 1) * 2 * P : 2],
-                            identity[:],
-                        )
-                copier = nc.vector.tensor_copy if g < VECTOR_COPIES else nc.scalar.copy
-                copier(
-                    out=grouped[:, g, :, :]
-                    .rearrange("p b k -> p (b k)")
-                    .bitcast(F32)
-                    .rearrange("p (b u) -> p b u", u=2),
-                    in_=pairs_ps[:].rearrange("p u b -> p b u"),
-                )
+                for u in range(2):
+                    nc.tensor.transpose(
+                        pairs_ps[:, g, u, :],
+                        pairs[:, g * 2 * P + u : (g + 1) * 2 * P : 2],
+                        identity[:],
+                    )
+            pairs_of[(e, t)] = pairs_ps
+
+        def group(e, t):
+            if e >= EXPERTS:
+                return
+            grouped = work.tile([P, PASSES, P, PACK], BF16, align_bytes=64)
+            copier = nc.vector.tensor_copy if (e, t) in VECTOR_COPIES else nc.scalar.copy
+            copier(
+                out=grouped[:]
+                .rearrange("p g b k -> p (g b k)")
+                .bitcast(F32)
+                .rearrange("p (g b u) -> p g b u", g=PASSES, u=2),
+                in_=pairs_of[(e, t)][:].rearrange("p g u b -> p g b u"),
+            )
+            grouped_of[(e, t)] = grouped
+
+        def quantise(e, t):
+            if e >= EXPERTS:
+                return
             nc.vector.quantize_mx(
-                out=h_words[:, e, :, :].rearrange("p g b -> p (g b)").bitcast(FP8X4),
-                scales=h_scales[:, e, :, :].rearrange("p g b -> p (g b)"),
-                in_=grouped[:].rearrange("p g b k -> p (g b k)"),
+                out=h_words[:, e, t, :, :].rearrange("p g b -> p (g b)").bitcast(FP8X4),
+                scales=h_scales[:, e, t, :, :].rearrange("p g b -> p (g b)"),
+                in_=grouped_of[(e, t)][:].rearrange("p g b k -> p (g b k)"),
             )
 
-        def expert_layer(e):
+        zT_of = {}
+
+        def blocks_layer(e):
+            if not 0 <= e < EXPERTS:
+                return
             for c in range(CHUNKS):
                 cols = slice(c * P, (c + 1) * P)
-                zT_ps = psum.tile([P, BATCH], F32, tag="out")
-                for g in range(PASSES):
-                    nc.tensor.matmul_mx(
-                        out=zT_ps[:],
-                        lhsT=w_words[:, e * PASSES + g, cols].bitcast(FP8X4),
-                        lhsT_scale=w_scales[:, e * PASSES + g, cols],
-                        rhs=h_words[:, e, g, :].bitcast(FP8X4),
-                        rhs_scale=h_scales[:, e, g, :],
-                        start=(g == 0),
-                        stop=(g == PASSES - 1),
-                    )
-                tiles = len([t for t in range(ROW_TILES) if tensor_width(c, t) > 0])
+                tiles = [t for t in range(ROW_TILES) if tensor_width(c, t) > 0]
+                zT_ps = psum.tile([P, len(tiles), P], F32, tag="out")
+                zT_of[(e, c)] = zT_ps
+                for t in tiles:
+                    for g in range(PASSES):
+                        nc.tensor.matmul_mx(
+                            out=zT_ps[:, t, :],
+                            lhsT=w_words[:, e * PASSES + g, cols].bitcast(FP8X4),
+                            lhsT_scale=w_scales[:, e * PASSES + g, cols],
+                            rhs=h_words[:, e, t, g, :].bitcast(FP8X4),
+                            rhs_scale=h_scales[:, e, t, g, :],
+                            start=(g == 0),
+                            stop=(g == PASSES - 1),
+                        )
+
+        def keep_blocks(e):
+            if not 0 <= e < EXPERTS:
+                return
+            for c in range(CHUNKS):
+                tiles = [t for t in range(ROW_TILES) if tensor_width(c, t) > 0]
                 nc.scalar.activation(
-                    out=zT_blocks[:, c, 0 : tiles * BLOCKS_PER_TILE, e, :],
-                    in_=zT_ps[:, 0 : tiles * P].rearrange("p (j i) -> p j i", i=ROWS_PER_BLOCK),
+                    out=zT_blocks[:, c, 0 : len(tiles) * BLOCKS_PER_TILE, e, :],
+                    in_=zT_of[(e, c)][:].rearrange("p t (j i) -> p (t j) i", i=ROWS_PER_BLOCK),
                     func=ACT.Identity,
                     bias=bias[:, c, e : e + 1],
                     scale=1.0,
                 )
-                if c >= VECTOR_CHUNK:
-                    nc.scalar.activation(
-                        out=zT_rows[:, c, e, :],
-                        in_=zT_ps[:, BATCH - P : BATCH],
-                        func=ACT.Identity,
-                        bias=bias[:, c, e : e + 1],
-                        scale=1.0,
-                    )
 
         row_chunks = CHUNKS - VECTOR_CHUNK
         skipped = VECTOR_FIRST - VECTOR_CHUNK * P
@@ -289,24 +333,59 @@ def tile_softmoedynamics_pb_e_kernel(tc, h2, logits, W3_words, W3_scales, b3, ou
         row_rounds = EXPERTS // experts_per_round
         y_rows = keep.tile([P, EXPERTS, VECTOR_COLS], F32)
         out_rows = keep.tile([P, AGENTS, VECTOR_COLS], F32)
+        bias_rows = keep.tile([P, EXPERTS, VECTOR_COLS], F32)
 
-        def spread_rows(r):
+        def spread_bias(r):
             first = r * experts_per_round
-            z_ps = psum.tile([P, experts_per_round, row_chunks, P], F32, tag="in")
+            bias_ps = psum.tile([P, experts_per_round, row_chunks, P], F32, tag="out")
             for e in range(first, first + experts_per_round):
                 for c in range(VECTOR_CHUNK, CHUNKS):
                     nc.tensor.transpose(
-                        z_ps[:, e - first, c - VECTOR_CHUNK, :], zT_rows[:, c, e, :], identity[:]
+                        bias_ps[:, e - first, c - VECTOR_CHUNK, :],
+                        bias[:, c, e : e + 1].to_broadcast([P, P]),
+                        identity[:],
                     )
-            z_of[("rows", r)] = [z_ps[:].rearrange("p e c l -> p e (c l)")[:, :, skipped:]]
-            y_of[("rows", r)] = [y_rows[:, first : first + experts_per_round, :]]
+            nc.vector.tensor_copy(
+                out=bias_rows[:, first : first + experts_per_round, :],
+                in_=bias_ps[:].rearrange("p e c l -> p e (c l)")[:, :, skipped:],
+            )
 
-        def weigh_expert(e):
-            for n in range(AGENTS):
+        rows_ps_of = {}
+
+        def rows_layer(e):
+            if e >= EXPERTS:
+                return
+            wide = slice(VECTOR_CHUNK * P, COLS)
+            z_ps = psum.tile([P, 1, row_chunks * P], F32, tag="out")
+            for g in range(PASSES):
+                nc.tensor.matmul_mx(
+                    out=z_ps[:, 0, :],
+                    lhsT=h_words[:, e, LAST, g, :].bitcast(FP8X4),
+                    lhsT_scale=h_scales[:, e, LAST, g, :],
+                    rhs=w_words[:, e * PASSES + g, wide].bitcast(FP8X4),
+                    rhs_scale=w_scales[:, e * PASSES + g, wide],
+                    start=(g == 0),
+                    stop=(g == PASSES - 1),
+                )
+            rows_ps_of[e] = z_ps
+
+        def add_bias(e):
+            z_rows = work.tile([P, 1, VECTOR_COLS], F32)
+            nc.vector.tensor_tensor(
+                out=z_rows[:],
+                in0=rows_ps_of[e][:, :, skipped:],
+                in1=bias_rows[:, e : e + 1, :],
+                op=ALU.add,
+            )
+            z_of[("rows", e)] = [z_rows[:]]
+            y_of[("rows", e)] = [y_rows[:, e : e + 1, :]]
+
+        def weigh(e, agents):
+            for n in agents if 0 <= e < EXPERTS else []:
                 weight = mix_rows[:, 0, n * EXPERTS + e : n * EXPERTS + e + 1]
                 if e == 0:
-                    nc.scalar.activation(
-                        out=out_rows[:, n, :], in_=y_rows[:, e, :], func=ACT.Identity, scale=weight
+                    nc.vector.tensor_scalar_mul(
+                        out=out_rows[:, n, :], in0=y_rows[:, e, :], scalar1=weight
                     )
                 else:
                     nc.vector.scalar_tensor_tensor(
@@ -370,64 +449,116 @@ def tile_softmoedynamics_pb_e_kernel(tc, h2, logits, W3_words, W3_scales, b3, ou
                     in_=out_blocks[:],
                 )
 
-        chain = ["mix rows", None]
-        for r in range(row_rounds):
-            chain.extend([("rows", r)] + [None] * (experts_per_round - 1))
-        first_rows = chain.index(("rows", 0))
-        chain[first_rows + 1] = "mix blocks"
-        first_blocks = len(chain) - (experts_per_round - 1)
-        chain = chain[0:first_blocks] + [("blocks", q) for q in range(len(block_items))]
+        chain = [("blocks", q) for q in range(len(block_items))]
 
         def item_at(k):
             return chain[k] if 0 <= k < len(chain) else None
 
-        def is_blocks(name):
-            return name is not None and name[0] == "blocks"
-
         def chain_step(k):
-            ahead, new, mid, old = [item_at(k + 1 - d) for d in range(4)]
-            weighed = k - first_rows - 1
-            if new is not None and new[0] == "rows":
-                spread_rows(new[1])
-            if is_blocks(ahead):
+            ahead, new, mid, old, older = [item_at(k + 1 - d) for d in range(5)]
+            if older is not None:
+                combine_blocks(older[1])
+            if ahead is not None:
                 spread_blocks(ahead[1])
-            if is_blocks(old):
-                combine_blocks(old[1])
+            find_tops(new, range(len(z_of[new])))
+            if old is not None:
+                place_blocks(old[1])
+                scale_powers(old, nc.gpsimd)
+            if mid is not None:
+                sum_powers(mid)
+            raise_powers(new, range(len(z_of[new])))
+            if mid is not None:
+                invert_sums(mid)
+
+        turn(0, LAST)
+        group(0, LAST)
+        quantise(0, LAST)
+        turn(0, 0)
+        group(0, 0)
+        find_tops("mix rows", [0])
+        transpose_bias()
+        quantise(0, 0)
+        raise_powers("mix rows")
+        rows_layer(0)
+        spread_bias(0)
+        turn(1, LAST)
+        group(1, LAST)
+        sum_powers("mix rows")
+        spread_bias(1)
+        turn(1, 0)
+        group(1, 0)
+        invert_sums("mix rows")
+        spread_bias(2)
+        spread_bias(3)
+        scale_powers("mix rows", nc.vector)
+
+        def rows_item(e):
+            return ("rows", e) if 0 <= e < EXPERTS else None
+
+        def early(e):
+            return e if e < EXPERTS - 2 else -1
+
+        for e in range(EXPERTS + 1):
+            new, mid = rows_item(e), rows_item(e - 1)
+            if e >= TURN_FIRST:
+                turn(e + 2, LAST)
+                turn(e + 2, 0)
+            if mid is not None:
+                exponentiate(mid)
+            keep_blocks(e - 1)
+            blocks_layer(e)
+            if new is not None:
+                add_bias(e)
+            quantise(e + 1, LAST)
+            rows_layer(e + 1)
+            if e < TURN_FIRST:
+                turn(e + 2, LAST)
+                turn(e + 2, 0)
+            group(e + 2, LAST)
+            group(e + 2, 0)
+            if mid is not None:
+                sum_powers(mid)
+            weigh(early(e - 2), [0, 1])
             if new is not None:
                 find_tops(new, [0])
             if mid is not None:
-                sum_powers(mid)
-            if new is not None:
-                find_tops(new, range(1, len(z_of[new])))
-            if 0 <= weighed < EXPERTS and weighed % experts_per_round > 0:
-                weigh_expert(weighed)
-            if weighed == EXPERTS - 1:
-                nc.sync.dma_start(
-                    out=out[BATCH - P : BATCH, :, VECTOR_FIRST:COLS], in_=out_rows[:]
-                )
-            if mid is not None:
                 invert_sums(mid)
-            by_gpsimd = is_blocks(mid) and mid != chain[-1]
-            if is_blocks(mid):
-                place_blocks(mid[1])
-            if by_gpsimd:
-                scale_powers(mid, nc.gpsimd)
+            weigh(early(e - 2), [2, 3])
             if new is not None:
-                raise_powers(new)
-            if mid is not None and not by_gpsimd:
+                raise_powers(new, later=True)
+            if mid is not None:
                 scale_powers(mid, nc.vector)
-            if mid == "mix blocks":
-                build_mix_blocks()
-            if 0 <= weighed < EXPERTS and weighed % experts_per_round == 0:
-                weigh_expert(weighed)
-
-        assert first_rows == experts_per_round
-        quantise_expert(0)
-        transpose_bias()
-        for e in range(EXPERTS):
-            if e + 1 < EXPERTS:
-                quantise_expert(e + 1)
-            expert_layer(e)
-            chain_step(e)
-        for k in range(EXPERTS, len(chain) + 2):
+            weigh(early(e - 2), [4, 5, 6, 7])
+            quantise(e + 1, 0)
+            if e == MIX_AT:
+                find_tops("mix blocks", [0])
+            if e == MIX_AT + 1:
+                raise_powers("mix blocks")
+            if e == MIX_AT + 2:
+                sum_powers("mix blocks")
+            if e == MIX_AT + 3:
+                invert_sums("mix blocks")
+            if e == MIX_AT + 4:
+                scale_powers("mix blocks", nc.vector)
+        spread_blocks(0)
+        order_mix()
+        for k in range(len(chain)):
             chain_step(k)
+            if k == 0:
+                build_mix_blocks()
+        last = len(block_items) - 1
+        combine_blocks(last - 2)
+        weigh(EXPERTS - 2, [0, 1, 2])
+        place_blocks(last - 1)
+        scale_powers(("blocks", last - 1), nc.vector)
+        combine_blocks(last - 1)
+        sum_powers(("blocks", last))
+        weigh(EXPERTS - 2, [3, 4, 5])
+        invert_sums(("blocks", last))
+        weigh(EXPERTS - 2, [6, 7])
+        weigh(EXPERTS - 1, [0])
+        place_blocks(last)
+        scale_powers(("blocks", last), nc.vector)
+        combine_blocks(last)
+        weigh(EXPERTS - 1, range(1, AGENTS))
+        nc.sync.dma_start(out=out[BATCH - P : BATCH, :, VECTOR_FIRST:COLS], in_=out_rows[:])

@@ -53,6 +53,9 @@ TURN_FIRST = 0
 VECTOR_COPIES = []
 
 
+STORE_AGENTS = 2
+
+
 def tile_softmoedynamics_pb_e_kernel(tc, h2, logits, W3_words, W3_scales, b3, out):
     nc = tc.nc
     with ExitStack() as ctx:
@@ -241,12 +244,19 @@ def tile_softmoedynamics_pb_e_kernel(tc, h2, logits, W3_words, W3_scales, b3, ou
                 mix_ei[:].rearrange("p e i -> p (e i)"),
                 identity[:],
             )
-            nc.vector.tensor_tensor(
-                out=mix_blocks[:],
-                in0=mix_ps[:].rearrange("p n j -> p j n").unsqueeze(2).to_broadcast(block_shape),
-                in1=same_row[:].unsqueeze(1).unsqueeze(3).to_broadcast(block_shape),
-                op=ALU.mult,
-            )
+            mix_turned = keep.tile([P, AGENTS, BLOCKS], F32)
+            nc.scalar.copy(out=mix_turned[:], in_=mix_ps[:])
+            tile_shape = [P, BLOCKS_PER_TILE, ROWS_PER_BLOCK, AGENTS]
+            for first in range(0, BLOCKS, BLOCKS_PER_TILE):
+                nc.gpsimd.tensor_tensor(
+                    out=mix_blocks[:, first : first + BLOCKS_PER_TILE, :, :],
+                    in0=mix_turned[:, :, first : first + BLOCKS_PER_TILE]
+                    .rearrange("p n j -> p j n")
+                    .unsqueeze(2)
+                    .to_broadcast(tile_shape),
+                    in1=same_row[:].unsqueeze(1).unsqueeze(3).to_broadcast(tile_shape),
+                    op=ALU.mult,
+                )
 
         h_words = keep.tile([P, EXPERTS, ROW_TILES, PASSES, P], U32, align_bytes=64)
         h_scales = keep.tile([P, EXPERTS, ROW_TILES, PASSES, P], U8, align_bytes=64)
@@ -559,6 +569,10 @@ def tile_softmoedynamics_pb_e_kernel(tc, h2, logits, W3_words, W3_scales, b3, ou
         weigh(EXPERTS - 1, [0])
         place_blocks(last)
         scale_powers(("blocks", last), nc.vector)
+        for first in range(0, AGENTS, STORE_AGENTS):
+            weigh(EXPERTS - 1, range(max(first, 1), first + STORE_AGENTS))
+            nc.sync.dma_start(
+                out=out[BATCH - P : BATCH, first : first + STORE_AGENTS, VECTOR_FIRST:COLS],
+                in_=out_rows[:, first : first + STORE_AGENTS, :],
+            )
         combine_blocks(last)
-        weigh(EXPERTS - 1, range(1, AGENTS))
-        nc.sync.dma_start(out=out[BATCH - P : BATCH, :, VECTOR_FIRST:COLS], in_=out_rows[:])

@@ -47,13 +47,14 @@ def tensor_width(c, t):
 
 
 LAST = ROW_TILES - 1
-LOGITS_AFTER = 3
-MIX_AT = 4
 TURN_FIRST = 0
 VECTOR_COPIES = []
 
 
 STORE_AGENTS = 2
+
+
+SPREAD_PARTS = 8
 
 
 def tile_softmoedynamics_pb_e_kernel(tc, h2, logits, W3_words, W3_scales, b3, out):
@@ -67,9 +68,9 @@ def tile_softmoedynamics_pb_e_kernel(tc, h2, logits, W3_words, W3_scales, b3, ou
         b3_rows = keep.tile([P, COLS], BF16)
         nc.vector.memset(b3_rows[:], 0.0)
         nc.scalar.dma_start(out=b3_rows[0:EXPERTS, :], in_=b3[:, :])
-        logit_rows = keep.tile([P, 1, AGENTS * EXPERTS], BF16)
+        logit_rows = keep.tile([P, ROW_TILES, AGENTS * EXPERTS], BF16)
         nc.scalar.dma_start(
-            out=logit_rows[:, 0, :], in_=logits[BATCH - P : BATCH].rearrange("b n e -> b (n e)")
+            out=logit_rows[:], in_=logits.rearrange("(t b) n e -> b t (n e)", b=P)
         )
 
         h2_rows = keep.tile([P, EXPERTS, ROW_TILES, FEATURES], BF16)
@@ -87,7 +88,6 @@ def tile_softmoedynamics_pb_e_kernel(tc, h2, logits, W3_words, W3_scales, b3, ou
                 in_=W3_words[passes].rearrange("g p n t -> p g (n t)").bitcast(I32),
             )
 
-        logit_blocks = keep.tile([P, 1, ROWS_PER_BLOCK * EXPERTS], BF16)
         for e in range(EXPERTS):
             load_rows(e, LAST)
             load_weights(e)
@@ -99,14 +99,6 @@ def tile_softmoedynamics_pb_e_kernel(tc, h2, logits, W3_words, W3_scales, b3, ou
                         in_=W3_scales[:, 4 * quadrant : 4 * quadrant + 4, :]
                         .rearrange("g r n -> r g n")
                         .bitcast(I32),
-                    )
-            if e == LOGITS_AFTER:
-                for n in range(AGENTS):
-                    nc.sync.dma_start(
-                        out=logit_blocks[n * BLOCKS : (n + 1) * BLOCKS, 0, :].rearrange(
-                            "j (i e) -> j i e", e=EXPERTS
-                        ),
-                        in_=logits[:, n, :].rearrange("(j i) e -> j i e", i=ROWS_PER_BLOCK),
                     )
         warm = keep.tile([P, 1], F32)
         nc.vector.memset(warm[:], 0.0)
@@ -215,47 +207,52 @@ def tile_softmoedynamics_pb_e_kernel(tc, h2, logits, W3_words, W3_scales, b3, ou
                 nc.tensor.transpose(b3_ps[:, c, :], b3_wide[:, c * P : (c + 1) * P], identity[:])
             nc.vector.tensor_copy(out=bias[:], in_=b3_ps[:, :, 0:EXPERTS])
 
-        mix_rows = keep.tile([P, 1, AGENTS * EXPERTS], F32)
+        mix_rows = keep.tile([P, ROW_TILES, AGENTS * EXPERTS], F32)
         z_of["mix rows"] = [logit_rows[:]]
         y_of["mix rows"] = [mix_rows[:]]
-        mix_ie = keep.tile([P, 1, ROWS_PER_BLOCK * EXPERTS], F32)
-        z_of["mix blocks"] = [logit_blocks[:]]
-        y_of["mix blocks"] = [mix_ie[:]]
-        block_shape = [P, BLOCKS, ROWS_PER_BLOCK, AGENTS]
-        mix_blocks = keep.tile(block_shape, F32)
+        mix_blocks = keep.tile([P, BLOCKS, ROWS_PER_BLOCK, AGENTS], F32)
         same_row = keep.tile([P, ROWS_PER_BLOCK], F32)
-        mix_ei = keep.tile([P, EXPERTS, ROWS_PER_BLOCK], F32)
+        weights = ROW_TILES * AGENTS * EXPERTS
+        mix_spread = keep.tile([P, weights, ROWS_PER_BLOCK], F32)
 
-        def order_mix():
+        def mark_rows():
             nc.vector.tensor_reduce(
                 out=same_row[:],
-                in_=identity[:].rearrange("p (e i) -> p i e", i=ROWS_PER_BLOCK),
+                in_=identity[:].rearrange("p (j i) -> p i j", i=ROWS_PER_BLOCK),
                 axis=AXIS.X,
                 op=ALU.add,
             )
-            nc.vector.tensor_copy(
-                out=mix_ei[:], in_=mix_ie[:, 0, :].rearrange("p (i e) -> p e i", e=EXPERTS)
-            )
 
-        def build_mix_blocks():
-            mix_ps = psum.tile([P, AGENTS, BLOCKS], F32, tag="out")
-            nc.tensor.transpose(
-                mix_ps[:].rearrange("p n j -> p (n j)"),
-                mix_ei[:].rearrange("p e i -> p (e i)"),
-                identity[:],
-            )
-            mix_turned = keep.tile([P, AGENTS, BLOCKS], F32)
-            nc.scalar.copy(out=mix_turned[:], in_=mix_ps[:])
-            tile_shape = [P, BLOCKS_PER_TILE, ROWS_PER_BLOCK, AGENTS]
-            for first in range(0, BLOCKS, BLOCKS_PER_TILE):
+        def spread_mix():
+            part = weights // SPREAD_PARTS
+            for first in range(0, weights, part):
+                shape = [P, part, ROWS_PER_BLOCK]
                 nc.gpsimd.tensor_tensor(
-                    out=mix_blocks[:, first : first + BLOCKS_PER_TILE, :, :],
-                    in0=mix_turned[:, :, first : first + BLOCKS_PER_TILE]
-                    .rearrange("p n j -> p j n")
+                    out=mix_spread[:, first : first + part, :],
+                    in0=mix_rows[:]
+                    .rearrange("p t w -> p (t w)")[:, first : first + part]
                     .unsqueeze(2)
-                    .to_broadcast(tile_shape),
-                    in1=same_row[:].unsqueeze(1).unsqueeze(3).to_broadcast(tile_shape),
+                    .to_broadcast(shape),
+                    in1=same_row[:].unsqueeze(1).to_broadcast(shape),
                     op=ALU.mult,
+                )
+
+        def build_mix_blocks(t):
+            per_bank = BANK // P
+            for first in range(0, AGENTS, per_bank):
+                mix_ps = psum.tile([P, per_bank, BLOCKS_PER_TILE, ROWS_PER_BLOCK], F32, tag="out")
+                for n in range(first, first + per_bank):
+                    at = (t * AGENTS + n) * EXPERTS
+                    nc.tensor.transpose(
+                        mix_ps[:, n - first, :, :].rearrange("p j i -> p (j i)"),
+                        mix_spread[:, at : at + EXPERTS, :].rearrange("p e i -> p (e i)"),
+                        identity[:],
+                    )
+                nc.scalar.copy(
+                    out=mix_blocks[
+                        :, t * BLOCKS_PER_TILE : (t + 1) * BLOCKS_PER_TILE, :, first : first + per_bank
+                    ],
+                    in_=mix_ps[:].rearrange("p n j i -> p j i n"),
                 )
 
         h_words = keep.tile([P, EXPERTS, ROW_TILES, PASSES, P], U32, align_bytes=64)
@@ -392,7 +389,7 @@ def tile_softmoedynamics_pb_e_kernel(tc, h2, logits, W3_words, W3_scales, b3, ou
 
         def weigh(e, agents):
             for n in agents if 0 <= e < EXPERTS else []:
-                weight = mix_rows[:, 0, n * EXPERTS + e : n * EXPERTS + e + 1]
+                weight = mix_rows[:, LAST, n * EXPERTS + e : n * EXPERTS + e + 1]
                 if e == 0:
                     nc.vector.tensor_scalar_mul(
                         out=out_rows[:, n, :], in0=y_rows[:, e, :], scalar1=weight
@@ -485,6 +482,7 @@ def tile_softmoedynamics_pb_e_kernel(tc, h2, logits, W3_words, W3_scales, b3, ou
         quantise(0, LAST)
         turn(0, 0)
         group(0, 0)
+        mark_rows()
         find_tops("mix rows", [0])
         transpose_bias()
         quantise(0, 0)
@@ -501,6 +499,7 @@ def tile_softmoedynamics_pb_e_kernel(tc, h2, logits, W3_words, W3_scales, b3, ou
         spread_bias(2)
         spread_bias(3)
         scale_powers("mix rows", nc.vector)
+        spread_mix()
 
         def rows_item(e):
             return ("rows", e) if 0 <= e < EXPERTS else None
@@ -540,22 +539,11 @@ def tile_softmoedynamics_pb_e_kernel(tc, h2, logits, W3_words, W3_scales, b3, ou
                 scale_powers(mid, nc.vector)
             weigh(early(e - 2), [4, 5, 6, 7])
             quantise(e + 1, 0)
-            if e == MIX_AT:
-                find_tops("mix blocks", [0])
-            if e == MIX_AT + 1:
-                raise_powers("mix blocks")
-            if e == MIX_AT + 2:
-                sum_powers("mix blocks")
-            if e == MIX_AT + 3:
-                invert_sums("mix blocks")
-            if e == MIX_AT + 4:
-                scale_powers("mix blocks", nc.vector)
         spread_blocks(0)
-        order_mix()
         for k in range(len(chain)):
             chain_step(k)
-            if k == 0:
-                build_mix_blocks()
+            if k < ROW_TILES:
+                build_mix_blocks(k)
         last = len(block_items) - 1
         combine_blocks(last - 2)
         weigh(EXPERTS - 2, [0, 1, 2])

@@ -54,7 +54,7 @@ VECTOR_COPIES = []
 STORE_AGENTS = 2
 
 
-SPREAD_PARTS = 8
+SPREAD_PARTS = 2
 
 
 def tile_softmoedynamics_pb_e_kernel(tc, h2, logits, W3_words, W3_scales, b3, out):
@@ -223,11 +223,11 @@ def tile_softmoedynamics_pb_e_kernel(tc, h2, logits, W3_words, W3_scales, b3, ou
                 op=ALU.add,
             )
 
-        def spread_mix():
+        def spread_mix(piece):
             part = weights // SPREAD_PARTS
-            for first in range(0, weights, part):
+            for first in [piece * part]:
                 shape = [P, part, ROWS_PER_BLOCK]
-                nc.gpsimd.tensor_tensor(
+                nc.vector.tensor_tensor(
                     out=mix_spread[:, first : first + part, :],
                     in0=mix_rows[:]
                     .rearrange("p t w -> p (t w)")[:, first : first + part]
@@ -499,7 +499,6 @@ def tile_softmoedynamics_pb_e_kernel(tc, h2, logits, W3_words, W3_scales, b3, ou
         spread_bias(2)
         spread_bias(3)
         scale_powers("mix rows", nc.vector)
-        spread_mix()
 
         def rows_item(e):
             return ("rows", e) if 0 <= e < EXPERTS else None
@@ -539,6 +538,8 @@ def tile_softmoedynamics_pb_e_kernel(tc, h2, logits, W3_words, W3_scales, b3, ou
                 scale_powers(mid, nc.vector)
             weigh(early(e - 2), [4, 5, 6, 7])
             quantise(e + 1, 0)
+            if e < SPREAD_PARTS:
+                spread_mix(e)
         spread_blocks(0)
         for k in range(len(chain)):
             chain_step(k)

@@ -352,7 +352,7 @@ def tile_softmoedynamics_pb_e_kernel(tc, h2, logits, W3_words, W3_scales, b3, ou
                         bias[:, c, e : e + 1].to_broadcast([P, P]),
                         identity[:],
                     )
-            nc.vector.tensor_copy(
+            nc.scalar.copy(
                 out=bias_rows[:, first : first + experts_per_round, :],
                 in_=bias_ps[:].rearrange("p e c l -> p e (c l)")[:, :, skipped:],
             )
@@ -471,34 +471,37 @@ def tile_softmoedynamics_pb_e_kernel(tc, h2, logits, W3_words, W3_scales, b3, ou
             if old is not None:
                 place_blocks(old[1])
                 scale_powers(old, nc.gpsimd)
+            raise_powers(new, [0])
             if mid is not None:
                 sum_powers(mid)
-            raise_powers(new, range(len(z_of[new])))
+            raise_powers(new, range(1, len(z_of[new])))
             if mid is not None:
                 invert_sums(mid)
 
         turn(0, LAST)
         group(0, LAST)
-        quantise(0, LAST)
-        turn(0, 0)
-        group(0, 0)
         mark_rows()
         find_tops("mix rows", [0])
-        transpose_bias()
-        quantise(0, 0)
+        quantise(0, LAST)
         raise_powers("mix rows")
+        turn(0, 0)
+        group(0, 0)
+        transpose_bias()
+        sum_powers("mix rows")
+        quantise(0, 0)
+        invert_sums("mix rows")
         rows_layer(0)
         spread_bias(0)
         turn(1, LAST)
         group(1, LAST)
-        sum_powers("mix rows")
         spread_bias(1)
+        scale_powers("mix rows", nc.vector)
         turn(1, 0)
         group(1, 0)
-        invert_sums("mix rows")
         spread_bias(2)
         spread_bias(3)
-        scale_powers("mix rows", nc.vector)
+        for piece in range(SPREAD_PARTS):
+            spread_mix(piece)
 
         def rows_item(e):
             return ("rows", e) if 0 <= e < EXPERTS else None
@@ -511,19 +514,16 @@ def tile_softmoedynamics_pb_e_kernel(tc, h2, logits, W3_words, W3_scales, b3, ou
             if e >= TURN_FIRST:
                 turn(e + 2, LAST)
                 turn(e + 2, 0)
-            if mid is not None:
-                exponentiate(mid)
             keep_blocks(e - 1)
-            blocks_layer(e)
             if new is not None:
                 add_bias(e)
             quantise(e + 1, LAST)
             rows_layer(e + 1)
+            blocks_layer(e)
             if e < TURN_FIRST:
                 turn(e + 2, LAST)
                 turn(e + 2, 0)
             group(e + 2, LAST)
-            group(e + 2, 0)
             if mid is not None:
                 sum_powers(mid)
             weigh(early(e - 2), [0, 1])
@@ -533,13 +533,12 @@ def tile_softmoedynamics_pb_e_kernel(tc, h2, logits, W3_words, W3_scales, b3, ou
                 invert_sums(mid)
             weigh(early(e - 2), [2, 3])
             if new is not None:
-                raise_powers(new, later=True)
+                raise_powers(new)
+            group(e + 2, 0)
             if mid is not None:
                 scale_powers(mid, nc.vector)
             weigh(early(e - 2), [4, 5, 6, 7])
             quantise(e + 1, 0)
-            if e < SPREAD_PARTS:
-                spread_mix(e)
         spread_blocks(0)
         for k in range(len(chain)):
             chain_step(k)

@@ -57,6 +57,9 @@ STORE_AGENTS = 2
 SPREAD_PARTS = 2
 
 
+OTHER_AGENTS = 1
+
+
 def tile_softmoedynamics_pb_e_kernel(tc, h2, logits, W3_words, W3_scales, b3, out):
     nc = tc.nc
     with ExitStack() as ctx:
@@ -404,6 +407,44 @@ def tile_softmoedynamics_pb_e_kernel(tc, h2, logits, W3_words, W3_scales, b3, ou
                         op1=ALU.add,
                     )
 
+        first_other = AGENTS - OTHER_AGENTS
+        products = keep.tile([P, EXPERTS, OTHER_AGENTS, VECTOR_COLS], F32)
+        halves = keep.tile([P, EXPERTS // 2, OTHER_AGENTS, VECTOR_COLS], F32)
+
+        def multiply_others(experts):
+            for e in experts:
+                for n in range(first_other, AGENTS):
+                    nc.scalar.activation(
+                        out=products[:, e, n - first_other, :],
+                        in_=y_rows[:, e, :],
+                        func=ACT.Identity,
+                        scale=mix_rows[:, LAST, n * EXPERTS + e : n * EXPERTS + e + 1],
+                    )
+
+        def add_others(level):
+            if level == 0:
+                nc.gpsimd.tensor_tensor(
+                    out=halves[:], in0=products[:, 0:4, :, :], in1=products[:, 4:8, :, :], op=ALU.add
+                )
+            if level == 1:
+                nc.gpsimd.tensor_tensor(
+                    out=products[:, 0:2, :, :],
+                    in0=halves[:, 0:2, :, :],
+                    in1=halves[:, 2:4, :, :],
+                    op=ALU.add,
+                )
+            if level == 2:
+                nc.gpsimd.tensor_tensor(
+                    out=out_rows[:, first_other:AGENTS, :],
+                    in0=products[:, 0, :, :],
+                    in1=products[:, 1, :, :],
+                    op=ALU.add,
+                )
+                nc.sync.dma_start(
+                    out=out[BATCH - P : BATCH, first_other:AGENTS, VECTOR_FIRST:COLS],
+                    in_=out_rows[:, first_other:AGENTS, :],
+                )
+
         out_flat = out.rearrange("b n l -> (b n) l")
         blocks_per_round = BANK // P
         rounds_per_item = BLOCKS_PER_TILE // blocks_per_round
@@ -537,30 +578,45 @@ def tile_softmoedynamics_pb_e_kernel(tc, h2, logits, W3_words, W3_scales, b3, ou
             group(e + 2, 0)
             if mid is not None:
                 scale_powers(mid, nc.vector)
-            weigh(early(e - 2), [4, 5, 6, 7])
+            weigh(early(e - 2), [4, 5, 6])
             quantise(e + 1, 0)
         spread_blocks(0)
+        multiply_others(range(0, EXPERTS // 2))
         for k in range(len(chain)):
             chain_step(k)
+            if k == 0:
+                multiply_others(range(EXPERTS // 2, EXPERTS))
+                add_others(0)
+            if k == 1:
+                add_others(1)
+                add_others(2)
             if k < ROW_TILES:
                 build_mix_blocks(k)
         last = len(block_items) - 1
+        kept = [(e, n) for e in range(EXPERTS - 2, EXPERTS) for n in range(first_other)]
+        filled = {"count": 0}
+
+        def fill(count):
+            for e, n in kept[filled["count"] : filled["count"] + count]:
+                weigh(e, [n])
+                begin = n - n % STORE_AGENTS
+                if e == EXPERTS - 1 and (n + 1 - begin == STORE_AGENTS or n + 1 == first_other):
+                    nc.sync.dma_start(
+                        out=out[BATCH - P : BATCH, begin : n + 1, VECTOR_FIRST:COLS],
+                        in_=out_rows[:, begin : n + 1, :],
+                    )
+            filled["count"] = filled["count"] + count
+
         combine_blocks(last - 2)
-        weigh(EXPERTS - 2, [0, 1, 2])
+        fill(3)
         place_blocks(last - 1)
         scale_powers(("blocks", last - 1), nc.vector)
         combine_blocks(last - 1)
         sum_powers(("blocks", last))
-        weigh(EXPERTS - 2, [3, 4, 5])
+        fill(3)
         invert_sums(("blocks", last))
-        weigh(EXPERTS - 2, [6, 7])
-        weigh(EXPERTS - 1, [0])
+        fill(3)
         place_blocks(last)
         scale_powers(("blocks", last), nc.vector)
-        for first in range(0, AGENTS, STORE_AGENTS):
-            weigh(EXPERTS - 1, range(max(first, 1), first + STORE_AGENTS))
-            nc.sync.dma_start(
-                out=out[BATCH - P : BATCH, first : first + STORE_AGENTS, VECTOR_FIRST:COLS],
-                in_=out_rows[:, first : first + STORE_AGENTS, :],
-            )
+        fill(len(kept) - filled["count"])
         combine_blocks(last)

@@ -47,16 +47,8 @@ def tensor_width(c, t):
 
 
 LAST = ROW_TILES - 1
-TURN_FIRST = 0
-VECTOR_COPIES = []
-
-
 STORE_AGENTS = 2
-
-
 SPREAD_PARTS = 2
-
-
 OTHER_AGENTS = 1
 
 
@@ -283,8 +275,7 @@ def tile_softmoedynamics_pb_e_kernel(tc, h2, logits, W3_words, W3_scales, b3, ou
             if e >= EXPERTS:
                 return
             grouped = work.tile([P, PASSES, P, PACK], BF16, align_bytes=64)
-            copier = nc.vector.tensor_copy if (e, t) in VECTOR_COPIES else nc.scalar.copy
-            copier(
+            nc.scalar.copy(
                 out=grouped[:]
                 .rearrange("p g b k -> p (g b k)")
                 .bitcast(F32)
@@ -446,39 +437,53 @@ def tile_softmoedynamics_pb_e_kernel(tc, h2, logits, W3_words, W3_scales, b3, ou
                 )
 
         out_flat = out.rearrange("b n l -> (b n) l")
-        blocks_per_round = BANK // P
-        rounds_per_item = BLOCKS_PER_TILE // blocks_per_round
-        block_items = [
-            (c, t) for c in range(CHUNKS) for t in range(ROW_TILES) if tensor_width(c, t) > 0
-        ]
-        block_items = sorted(block_items, key=lambda ct: -tensor_width(ct[0], ct[1]))
+        rounds_per_item = 2
+
+        def tensor_columns(t):
+            return sum(tensor_width(c, t) for c in range(CHUNKS))
+
+        def blocks_per_round_of(t):
+            return BANK // (P * len([c for c in range(CHUNKS) if tensor_width(c, t) > 0]))
+
+        block_items = []
+        for t in range(ROW_TILES - 1, -1, -1):
+            blocks_per_item = rounds_per_item * blocks_per_round_of(t)
+            block_items.extend([(t, j) for j in range(0, BLOCKS_PER_TILE, blocks_per_item)])
+
+        def rounds_of(q):
+            t, begin = block_items[q]
+            count = blocks_per_round_of(t)
+            start = t * BLOCKS_PER_TILE + begin
+            return [start + v * count for v in range(rounds_per_item)], count
 
         def spread_blocks(q):
-            c, t = block_items[q]
-            width = tensor_width(c, t)
+            t = block_items[q][0]
+            firsts, count = rounds_of(q)
+            chunks = [c for c in range(CHUNKS) if tensor_width(c, t) > 0]
             views = []
-            for v in range(rounds_per_item):
-                first = t * BLOCKS_PER_TILE + v * blocks_per_round
-                z_ps = psum.tile([P, blocks_per_round, P], F32, tag="in")
-                for j in range(first, first + blocks_per_round):
-                    nc.tensor.transpose(
-                        z_ps[:, j - first, :],
-                        zT_blocks[:, c, j, :, :].rearrange("p e i -> p (e i)"),
-                        identity[:],
-                    )
-                views.append(z_ps[:, :, 0:width])
+            for first in firsts:
+                z_ps = psum.tile([P, count, len(chunks) * P], F32, tag="in")
+                for j in range(first, first + count):
+                    for c in chunks:
+                        nc.tensor.transpose(
+                            z_ps[:, j - first, c * P : (c + 1) * P],
+                            zT_blocks[:, c, j, :, :].rearrange("p e i -> p (e i)"),
+                            identity[:],
+                        )
+                views.append(z_ps[:, :, 0 : tensor_columns(t)])
             z_of[("blocks", q)] = views
 
         def place_blocks(q):
-            c, t = block_items[q]
-            y_blocks = work.tile([P, rounds_per_item, blocks_per_round, tensor_width(c, t)], F32)
+            t = block_items[q][0]
+            count = rounds_of(q)[1]
+            y_blocks = work.tile([P, rounds_per_item, count, tensor_columns(t)], F32)
             y_of[("blocks", q)] = [y_blocks[:, v, :, :] for v in range(rounds_per_item)]
 
         def combine_blocks(q):
-            c, t = block_items[q]
-            width = tensor_width(c, t)
+            width = tensor_columns(block_items[q][0])
+            firsts, blocks_per_round = rounds_of(q)
             for v in range(rounds_per_item):
-                first = t * BLOCKS_PER_TILE + v * blocks_per_round
+                first = firsts[v]
                 sum_ps = psum.tile([P, blocks_per_round, width], F32, tag="out")
                 for j in range(first, first + blocks_per_round):
                     nc.tensor.matmul(
@@ -492,7 +497,7 @@ def tile_softmoedynamics_pb_e_kernel(tc, h2, logits, W3_words, W3_scales, b3, ou
                 nc.scalar.copy(out=out_blocks[:], in_=sum_ps[:])
                 nc.sync.dma_start(
                     out=out_flat[
-                        first * P : (first + blocks_per_round) * P, c * P : c * P + width
+                        first * P : (first + blocks_per_round) * P, 0:width
                     ].rearrange("(j m) l -> m j l", m=P),
                     in_=out_blocks[:],
                 )
@@ -552,18 +557,14 @@ def tile_softmoedynamics_pb_e_kernel(tc, h2, logits, W3_words, W3_scales, b3, ou
 
         for e in range(EXPERTS + 1):
             new, mid = rows_item(e), rows_item(e - 1)
-            if e >= TURN_FIRST:
-                turn(e + 2, LAST)
-                turn(e + 2, 0)
+            turn(e + 2, LAST)
+            turn(e + 2, 0)
             keep_blocks(e - 1)
             if new is not None:
                 add_bias(e)
             quantise(e + 1, LAST)
             rows_layer(e + 1)
             blocks_layer(e)
-            if e < TURN_FIRST:
-                turn(e + 2, LAST)
-                turn(e + 2, 0)
             group(e + 2, LAST)
             if mid is not None:
                 sum_powers(mid)
@@ -591,7 +592,7 @@ def tile_softmoedynamics_pb_e_kernel(tc, h2, logits, W3_words, W3_scales, b3, ou
                 add_others(1)
                 add_others(2)
             if k < ROW_TILES:
-                build_mix_blocks(k)
+                build_mix_blocks(ROW_TILES - 1 - k)
         last = len(block_items) - 1
         kept = [(e, n) for e in range(EXPERTS - 2, EXPERTS) for n in range(first_other)]
         filled = {"count": 0}

@@ -50,6 +50,7 @@ LAST = ROW_TILES - 1
 STORE_AGENTS = 2
 SPREAD_PARTS = 2
 OTHER_AGENTS = 1
+STEP_WEIGHINGS = 6
 
 
 def tile_softmoedynamics_pb_e_kernel(tc, h2, logits, W3_words, W3_scales, b3, out):
@@ -62,11 +63,11 @@ def tile_softmoedynamics_pb_e_kernel(tc, h2, logits, W3_words, W3_scales, b3, ou
 
         b3_rows = keep.tile([P, COLS], BF16)
         nc.vector.memset(b3_rows[:], 0.0)
-        nc.scalar.dma_start(out=b3_rows[0:EXPERTS, :], in_=b3[:, :])
         logit_rows = keep.tile([P, ROW_TILES, AGENTS * EXPERTS], BF16)
         nc.scalar.dma_start(
             out=logit_rows[:], in_=logits.rearrange("(t b) n e -> b t (n e)", b=P)
         )
+        nc.scalar.dma_start(out=b3_rows[0:EXPERTS, :], in_=b3[:, :])
 
         h2_rows = keep.tile([P, EXPERTS, ROW_TILES, FEATURES], BF16)
         w_words = keep.tile([P, EXPERTS * PASSES, COLS], U32, align_bytes=64)
@@ -103,7 +104,6 @@ def tile_softmoedynamics_pb_e_kernel(tc, h2, logits, W3_words, W3_scales, b3, ou
         make_identity(nc, identity[:])
 
         b3_wide = keep.tile([P, COLS], F32)
-        nc.vector.tensor_copy(out=b3_wide[:], in_=b3_rows[:])
 
         z_of = {}
         y_of = {}
@@ -495,7 +495,8 @@ def tile_softmoedynamics_pb_e_kernel(tc, h2, logits, W3_words, W3_scales, b3, ou
                     )
                 out_blocks = work.tile([P, blocks_per_round, width], F32)
                 nc.scalar.copy(out=out_blocks[:], in_=sum_ps[:])
-                nc.sync.dma_start(
+                queue = nc.scalar if q == len(block_items) - 1 else nc.sync
+                queue.dma_start(
                     out=out_flat[
                         first * P : (first + blocks_per_round) * P, 0:width
                     ].rearrange("(j m) l -> m j l", m=P),
@@ -524,36 +525,43 @@ def tile_softmoedynamics_pb_e_kernel(tc, h2, logits, W3_words, W3_scales, b3, ou
             if mid is not None:
                 invert_sums(mid)
 
+        find_tops("mix rows", [0])
+        mark_rows()
+        raise_powers("mix rows")
+        nc.vector.tensor_copy(out=b3_wide[:], in_=b3_rows[:])
         turn(0, LAST)
         group(0, LAST)
-        mark_rows()
-        find_tops("mix rows", [0])
+        sum_powers("mix rows")
+        transpose_bias()
+        invert_sums("mix rows")
         quantise(0, LAST)
-        raise_powers("mix rows")
+        scale_powers("mix rows", nc.vector)
         turn(0, 0)
         group(0, 0)
-        transpose_bias()
-        sum_powers("mix rows")
+        spread_mix(0)
         quantise(0, 0)
-        invert_sums("mix rows")
         rows_layer(0)
         spread_bias(0)
         turn(1, LAST)
         group(1, LAST)
         spread_bias(1)
-        scale_powers("mix rows", nc.vector)
+        spread_mix(1)
         turn(1, 0)
         group(1, 0)
         spread_bias(2)
         spread_bias(3)
-        for piece in range(SPREAD_PARTS):
-            spread_mix(piece)
 
         def rows_item(e):
             return ("rows", e) if 0 <= e < EXPERTS else None
 
-        def early(e):
-            return e if e < EXPERTS - 2 else -1
+        early = [(e, n) for e in range(EXPERTS - 2) for n in range(first_other)]
+        weighed = {"count": 0}
+
+        def weigh_early(step, count):
+            for e, n in early[weighed["count"] : weighed["count"] + count]:
+                if e <= step - 2:
+                    weigh(e, [n])
+                    weighed["count"] = weighed["count"] + 1
 
         for e in range(EXPERTS + 1):
             new, mid = rows_item(e), rows_item(e - 1)
@@ -568,18 +576,18 @@ def tile_softmoedynamics_pb_e_kernel(tc, h2, logits, W3_words, W3_scales, b3, ou
             group(e + 2, LAST)
             if mid is not None:
                 sum_powers(mid)
-            weigh(early(e - 2), [0, 1])
+            weigh_early(e, 2)
             if new is not None:
                 find_tops(new, [0])
             if mid is not None:
                 invert_sums(mid)
-            weigh(early(e - 2), [2, 3])
+            weigh_early(e, 2)
             if new is not None:
                 raise_powers(new)
             group(e + 2, 0)
             if mid is not None:
                 scale_powers(mid, nc.vector)
-            weigh(early(e - 2), [4, 5, 6])
+            weigh_early(e, STEP_WEIGHINGS - 4)
             quantise(e + 1, 0)
         spread_blocks(0)
         multiply_others(range(0, EXPERTS // 2))
@@ -608,16 +616,13 @@ def tile_softmoedynamics_pb_e_kernel(tc, h2, logits, W3_words, W3_scales, b3, ou
                     )
             filled["count"] = filled["count"] + count
 
-        combine_blocks(last - 2)
-        fill(3)
         place_blocks(last - 1)
-        scale_powers(("blocks", last - 1), nc.vector)
-        combine_blocks(last - 1)
+        scale_powers(("blocks", last - 1), nc.gpsimd)
+        combine_blocks(last - 2)
         sum_powers(("blocks", last))
-        fill(3)
         invert_sums(("blocks", last))
-        fill(3)
         place_blocks(last)
         scale_powers(("blocks", last), nc.vector)
+        combine_blocks(last - 1)
         fill(len(kept) - filled["count"])
         combine_blocks(last)

@@ -50,6 +50,7 @@ LAST = ROW_TILES - 1
 STORE_AGENTS = 2
 SPREAD_PARTS = 2
 OTHER_AGENTS = 1
+GPSIMD_SUMS = 1
 STEP_WEIGHINGS = 6
 
 
@@ -151,6 +152,27 @@ def tile_softmoedynamics_pb_e_kernel(tc, h2, logits, W3_words, W3_scales, b3, ou
         def exponentiate(name):
             powers = powers_of[name]
             nc.scalar.activation(out=powers[:], in_=powers[:], func=ACT.Exp)
+
+        def sum_on_gpsimd(name):
+            powers = powers_of[name]
+            groups = powers.shape[1] * powers.shape[2] * powers.shape[3]
+            terms = powers[:].rearrange("p v a g i -> p (v a g) i")
+            fours = work.tile([P, groups, 4], F32)
+            nc.gpsimd.tensor_tensor(
+                out=fours[:], in0=terms[:, :, 0:4], in1=terms[:, :, 4:8], op=ALU.add
+            )
+            twos = work.tile([P, groups, 2], F32)
+            nc.gpsimd.tensor_tensor(
+                out=twos[:], in0=fours[:, :, 0:2], in1=fours[:, :, 2:4], op=ALU.add
+            )
+            total = work.tile([P, powers.shape[1], powers.shape[2], powers.shape[3]], F32, tag="sums")
+            nc.gpsimd.tensor_tensor(
+                out=total[:].rearrange("p v a g -> p (v a g)").unsqueeze(2),
+                in0=twos[:, :, 0:1],
+                in1=twos[:, :, 1:2],
+                op=ALU.add,
+            )
+            total_of[name] = total
 
         def sum_powers(name):
             powers = powers_of[name]
@@ -510,20 +532,24 @@ def tile_softmoedynamics_pb_e_kernel(tc, h2, logits, W3_words, W3_scales, b3, ou
 
         def chain_step(k):
             ahead, new, mid, old, older = [item_at(k + 1 - d) for d in range(5)]
-            if older is not None:
-                combine_blocks(older[1])
             if ahead is not None:
                 spread_blocks(ahead[1])
             find_tops(new, range(len(z_of[new])))
-            if old is not None:
+            if old is not None and old[1] >= GPSIMD_SUMS:
                 place_blocks(old[1])
                 scale_powers(old, nc.gpsimd)
             raise_powers(new, [0])
-            if mid is not None:
+            if mid is not None and mid[1] >= GPSIMD_SUMS:
                 sum_powers(mid)
             raise_powers(new, range(1, len(z_of[new])))
-            if mid is not None:
+            if mid is not None and mid[1] >= GPSIMD_SUMS:
                 invert_sums(mid)
+            if old is not None and old[1] < GPSIMD_SUMS:
+                invert_sums(old)
+                place_blocks(old[1])
+                scale_powers(old, nc.gpsimd)
+            if older is not None:
+                combine_blocks(older[1])
 
         find_tops("mix rows", [0])
         mark_rows()
@@ -593,14 +619,18 @@ def tile_softmoedynamics_pb_e_kernel(tc, h2, logits, W3_words, W3_scales, b3, ou
         multiply_others(range(0, EXPERTS // 2))
         for k in range(len(chain)):
             chain_step(k)
+            if k < GPSIMD_SUMS:
+                sum_on_gpsimd(chain[k])
             if k == 0:
                 multiply_others(range(EXPERTS // 2, EXPERTS))
                 add_others(0)
             if k == 1:
                 add_others(1)
                 add_others(2)
-            if k < ROW_TILES:
-                build_mix_blocks(ROW_TILES - 1 - k)
+            if k == 1:
+                build_mix_blocks(LAST)
+            if k == 2:
+                build_mix_blocks(0)
         last = len(block_items) - 1
         kept = [(e, n) for e in range(EXPERTS - 2, EXPERTS) for n in range(first_other)]
         filled = {"count": 0}

from contextlib import ExitStack

import concourse.mybir as mybir
from concourse.masks import make_identity

F32 = mybir.dt.float32
BF16 = mybir.dt.bfloat16
I32 = mybir.dt.int32
U32 = mybir.dt.uint32
U8 = mybir.dt.uint8
FP8X4 = mybir.dt.float8_e4m3fn_x4
ALU = mybir.AluOpType
ACT = mybir.ActivationFunctionType
AXIS = mybir.AxisListType

P = 128
PACK = 4
K_PASS = P * PACK
BANK = 512

BATCH = 256
EXPERTS = 8
AGENTS = 8
FEATURES = 1024
COLS = 384
GROUP = 8

PASSES = FEATURES // K_PASS
ROW_TILES = BATCH // P
CHUNKS = COLS // P

MX_FLOPS = 2 * BATCH * EXPERTS * FEATURES * COLS
FLOPS = MX_FLOPS + 2 * BATCH * AGENTS * EXPERTS * COLS

ROWS_PER_BLOCK = P // EXPERTS
BLOCKS = BATCH // ROWS_PER_BLOCK
BLOCKS_PER_TILE = P // ROWS_PER_BLOCK
VECTOR_COLS = 160
assert 10 * (2 * P * AGENTS * (BATCH * COLS - P * VECTOR_COLS)) <= MX_FLOPS
VECTOR_FIRST = COLS - VECTOR_COLS
VECTOR_CHUNK = VECTOR_FIRST // P


def tensor_width(c, t):
    last = COLS if t < ROW_TILES - 1 else VECTOR_FIRST
    return max(0, min(P, last - c * P))


LAST = ROW_TILES - 1
STORE_AGENTS = 2
SPREAD_PARTS = 2
OTHER_AGENTS = 1
GPSIMD_SUMS = 1
STEP_WEIGHINGS = 6


def tile_softmoedynamics_pb_e_kernel(tc, h2, logits, W3_words, W3_scales, b3, out):
    nc = tc.nc
    with ExitStack() as ctx:
        keep = ctx.enter_context(tc.tile_pool(name="keep", bufs=1))
        work = ctx.enter_context(tc.tile_pool(name="work", bufs=4))
        psum = ctx.enter_context(tc.psum_pool(name="psum", bufs=4))
        ctx.enter_context(tc.manual_schedule())

        b3_rows = keep.tile([P, COLS], BF16)
        nc.vector.memset(b3_rows[:], 0.0)
        logit_rows = keep.tile([P, ROW_TILES, AGENTS * EXPERTS], BF16)
        nc.scalar.dma_start(
            out=logit_rows[:], in_=logits.rearrange("(t b) n e -> b t (n e)", b=P)
        )
        nc.scalar.dma_start(out=b3_rows[0:EXPERTS, :], in_=b3[:, :])

        h2_rows = keep.tile([P, EXPERTS, ROW_TILES, FEATURES], BF16)
        w_words = keep.tile([P, EXPERTS * PASSES, COLS], U32, align_bytes=64)
        w_scales = keep.tile([P, EXPERTS * PASSES, COLS], U8, align_bytes=64)
        nc.vector.memset(w_scales[:].bitcast(I32), 0)

        def load_rows(e, t):
            nc.sync.dma_start(out=h2_rows[:, e, t, :], in_=h2[t * P : (t + 1) * P, e, :])

        def load_weights(e):
            passes = slice(e * PASSES, (e + 1) * PASSES)
            nc.sync.dma_start(
                out=w_words[:, passes, :].bitcast(I32),
                in_=W3_words[passes].rearrange("g p n t -> p g (n t)").bitcast(I32),
            )

        for e in range(EXPERTS):
            load_rows(e, LAST)
            load_weights(e)
            load_rows(e, 0)
            if e == 0:
                for quadrant in range(4):
                    nc.sync.dma_start(
                        out=w_scales[32 * quadrant : 32 * quadrant + 4, :, :].bitcast(I32),
                        in_=W3_scales[:, 4 * quadrant : 4 * quadrant + 4, :]
                        .rearrange("g r n -> r g n")
                        .bitcast(I32),
                    )
        warm = keep.tile([P, 1], F32)
        nc.vector.memset(warm[:], 0.0)
        nc.scalar.activation(out=warm[:], in_=warm[:], func=ACT.Exp)

        identity = keep.tile([P, P], F32)
        make_identity(nc, identity[:])

        b3_wide = keep.tile([P, COLS], F32)

        z_of = {}
        y_of = {}
        top_of = {}
        powers_of = {}
        total_of = {}
        inverse_of = {}

        def by_group(ap):
            return ap.rearrange("p a (g i) -> p a g i", i=GROUP)

        def over_group(ap):
            return ap.unsqueeze(3).to_broadcast([P, ap.shape[1], ap.shape[2], GROUP])

        def find_tops(name, which):
            views = z_of[name]
            if 0 in which:
                top = work.tile([P, len(views), views[0].shape[1], views[0].shape[2] // GROUP], F32)
                top_of[name] = top
            for v in which:
                nc.vector.tensor_reduce(
                    out=top_of[name][:, v, :, :], in_=by_group(views[v]), axis=AXIS.X, op=ALU.max
                )

        def raise_powers(name, which=(0,), later=False):
            views = z_of[name]
            top = top_of[name]
            shape = [P, len(views), views[0].shape[1], views[0].shape[2] // GROUP, GROUP]
            if 0 in which:
                powers = work.tile(shape, F32)
                powers_of[name] = powers
            powers = powers_of[name]
            for v in which:
                nc.vector.tensor_tensor(
                    out=powers[:, v, :, :, :],
                    in0=by_group(views[v]),
                    in1=over_group(top[:, v, :, :]),
                    op=ALU.subtract,
                )
                if not later:
                    nc.scalar.activation(
                        out=powers[:, v, :, :, :], in_=powers[:, v, :, :, :], func=ACT.Exp
                    )

        def exponentiate(name):
            powers = powers_of[name]
            nc.scalar.activation(out=powers[:], in_=powers[:], func=ACT.Exp)

        def sum_on_gpsimd(name):
            powers = powers_of[name]
            groups = powers.shape[1] * powers.shape[2] * powers.shape[3]
            terms = powers[:].rearrange("p v a g i -> p (v a g) i")
            fours = work.tile([P, groups, 4], F32)
            nc.gpsimd.tensor_tensor(
                out=fours[:], in0=terms[:, :, 0:4], in1=terms[:, :, 4:8], op=ALU.add
            )
            twos = work.tile([P, groups, 2], F32)
            nc.gpsimd.tensor_tensor(
                out=twos[:], in0=fours[:, :, 0:2], in1=fours[:, :, 2:4], op=ALU.add
            )
            total = work.tile([P, powers.shape[1], powers.shape[2], powers.shape[3]], F32, tag="sums")
            nc.gpsimd.tensor_tensor(
                out=total[:].rearrange("p v a g -> p (v a g)").unsqueeze(2),
                in0=twos[:, :, 0:1],
                in1=twos[:, :, 1:2],
                op=ALU.add,
            )
            total_of[name] = total

        def sum_powers(name):
            powers = powers_of[name]
            total = work.tile([P, powers.shape[1], powers.shape[2], powers.shape[3]], F32)
            nc.vector.tensor_reduce(
                out=total[:].rearrange("p v a g -> p (v a g)"),
                in_=powers[:].rearrange("p v a g i -> p (v a g) i"),
                axis=AXIS.X,
                op=ALU.add,
            )
            total_of[name] = total

        minus_one = keep.tile([P, 1], F32)
        nc.vector.memset(minus_one[:], -1.0)

        def invert_sums(name, by_gpsimd=False):
            total = total_of[name]
            inverse = work.tile([P, total.shape[1], total.shape[2], total.shape[3]], F32)
            count = total.shape[1] * total.shape[2] * total.shape[3]
            if by_gpsimd:
                nc.gpsimd.tensor_tensor(
                    out=inverse[:].rearrange("p v a g -> p (v a g)"),
                    in0=total[:].rearrange("p v a g -> p (v a g)"),
                    in1=minus_one[:].to_broadcast([P, count]),
                    op=ALU.pow,
                )
            else:
                nc.vector.reciprocal(
                    out=inverse[:].rearrange("p v a g -> p (v a g)"),
                    in_=total[:].rearrange("p v a g -> p (v a g)"),
                )
            inverse_of[name] = inverse

        def scale_powers(name, engine):
            places = y_of[name]
            for v in range(len(places)):
                engine.tensor_tensor(
                    out=by_group(places[v]),
                    in0=powers_of[name][:, v, :, :, :],
                    in1=over_group(inverse_of[name][:, v, :, :]),
                    op=ALU.mult,
                )

        bias = keep.tile([P, CHUNKS, EXPERTS], F32)

        def transpose_bias():
            b3_ps = psum.tile([P, CHUNKS, P], F32, tag="out")
            for c in range(CHUNKS):
                nc.tensor.transpose(b3_ps[:, c, :], b3_wide[:, c * P : (c + 1) * P], identity[:])
            nc.vector.tensor_copy(out=bias[:], in_=b3_ps[:, :, 0:EXPERTS])

        mix_rows = keep.tile([P, ROW_TILES, AGENTS * EXPERTS], F32)
        z_of["mix rows"] = [logit_rows[:]]
        y_of["mix rows"] = [mix_rows[:]]
        mix_blocks = keep.tile([P, BLOCKS, ROWS_PER_BLOCK, AGENTS], F32)
        same_row = keep.tile([P, ROWS_PER_BLOCK], F32)
        weights = ROW_TILES * AGENTS * EXPERTS
        mix_spread = keep.tile([P, weights, ROWS_PER_BLOCK], F32)

        def mark_rows():
            nc.vector.tensor_reduce(
                out=same_row[:],
                in_=identity[:].rearrange("p (j i) -> p i j", i=ROWS_PER_BLOCK),
                axis=AXIS.X,
                op=ALU.add,
            )

        def spread_mix(piece):
            part = weights // SPREAD_PARTS
            for first in [piece * part]:
                shape = [P, part, ROWS_PER_BLOCK]
                nc.vector.tensor_tensor(
                    out=mix_spread[:, first : first + part, :],
                    in0=mix_rows[:]
                    .rearrange("p t w -> p (t w)")[:, first : first + part]
                    .unsqueeze(2)
                    .to_broadcast(shape),
                    in1=same_row[:].unsqueeze(1).to_broadcast(shape),
                    op=ALU.mult,
                )

        def build_mix_blocks(t):
            per_bank = BANK // P
            for first in range(0, AGENTS, per_bank):
                mix_ps = psum.tile([P, per_bank, BLOCKS_PER_TILE, ROWS_PER_BLOCK], F32, tag="out")
                for n in range(first, first + per_bank):
                    at = (t * AGENTS + n) * EXPERTS
                    nc.tensor.transpose(
                        mix_ps[:, n - first, :, :].rearrange("p j i -> p (j i)"),
                        mix_spread[:, at : at + EXPERTS, :].rearrange("p e i -> p (e i)"),
                        identity[:],
                    )
                nc.scalar.copy(
                    out=mix_blocks[
                        :, t * BLOCKS_PER_TILE : (t + 1) * BLOCKS_PER_TILE, :, first : first + per_bank
                    ],
                    in_=mix_ps[:].rearrange("p n j i -> p j i n"),
                )

        h_words = keep.tile([P, EXPERTS, ROW_TILES, PASSES, P], U32, align_bytes=64)
        h_scales = keep.tile([P, EXPERTS, ROW_TILES, PASSES, P], U8, align_bytes=64)
        zT_blocks = keep.tile([P, CHUNKS, BLOCKS, EXPERTS, ROWS_PER_BLOCK], F32)

        pairs_of = {}
        grouped_of = {}

        def turn(e, t):
            if e >= EXPERTS:
                return
            pairs = h2_rows[:, e, t, :].bitcast(F32)
            pairs_ps = psum.tile([P, PASSES, 2, P], F32, tag="in")
            for g in range(PASSES):
                for u in range(2):
                    nc.tensor.transpose(
                        pairs_ps[:, g, u, :],
                        pairs[:, g * 2 * P + u : (g + 1) * 2 * P : 2],
                        identity[:],
                    )
            pairs_of[(e, t)] = pairs_ps

        def group(e, t):
            if e >= EXPERTS:
                return
            grouped = work.tile([P, PASSES, P, PACK], BF16, align_bytes=64)
            nc.scalar.copy(
                out=grouped[:]
                .rearrange("p g b k -> p (g b k)")
                .bitcast(F32)
                .rearrange("p (g b u) -> p g b u", g=PASSES, u=2),
                in_=pairs_of[(e, t)][:].rearrange("p g u b -> p g b u"),
            )
            grouped_of[(e, t)] = grouped

        def quantise(e, t):
            if e >= EXPERTS:
                return
            nc.vector.quantize_mx(
                out=h_words[:, e, t, :, :].rearrange("p g b -> p (g b)").bitcast(FP8X4),
                scales=h_scales[:, e, t, :, :].rearrange("p g b -> p (g b)"),
                in_=grouped_of[(e, t)][:].rearrange("p g b k -> p (g b k)"),
            )

        zT_of = {}

        def blocks_layer(e):
            if not 0 <= e < EXPERTS:
                return
            for c in range(CHUNKS):
                cols = slice(c * P, (c + 1) * P)
                tiles = [t for t in range(ROW_TILES) if tensor_width(c, t) > 0]
                zT_ps = psum.tile([P, len(tiles), P], F32, tag="out")
                zT_of[(e, c)] = zT_ps
                for t in tiles:
                    for g in range(PASSES):
                        nc.tensor.matmul_mx(
                            out=zT_ps[:, t, :],
                            lhsT=w_words[:, e * PASSES + g, cols].bitcast(FP8X4),
                            lhsT_scale=w_scales[:, e * PASSES + g, cols],
                            rhs=h_words[:, e, t, g, :].bitcast(FP8X4),
                            rhs_scale=h_scales[:, e, t, g, :],
                            start=(g == 0),
                            stop=(g == PASSES - 1),
                        )

        def keep_blocks(e):
            if not 0 <= e < EXPERTS:
                return
            for c in range(CHUNKS):
                tiles = [t for t in range(ROW_TILES) if tensor_width(c, t) > 0]
                nc.scalar.activation(
                    out=zT_blocks[:, c, 0 : len(tiles) * BLOCKS_PER_TILE, e, :],
                    in_=zT_of[(e, c)][:].rearrange("p t (j i) -> p (t j) i", i=ROWS_PER_BLOCK),
                    func=ACT.Identity,
                    bias=bias[:, c, e : e + 1],
                    scale=1.0,
                )

        row_chunks = CHUNKS - VECTOR_CHUNK
        skipped = VECTOR_FIRST - VECTOR_CHUNK * P
        experts_per_round = BANK // (row_chunks * P)
        row_rounds = EXPERTS // experts_per_round
        y_rows = keep.tile([P, EXPERTS, VECTOR_COLS], F32)
        out_rows = keep.tile([P, AGENTS, VECTOR_COLS], F32)
        bias_rows = keep.tile([P, EXPERTS, VECTOR_COLS], F32)

        def spread_bias(r):
            first = r * experts_per_round
            bias_ps = psum.tile([P, experts_per_round, row_chunks, P], F32, tag="out")
            for e in range(first, first + experts_per_round):
                for c in range(VECTOR_CHUNK, CHUNKS):
                    nc.tensor.transpose(
                        bias_ps[:, e - first, c - VECTOR_CHUNK, :],
                        bias[:, c, e : e + 1].to_broadcast([P, P]),
                        identity[:],
                    )
            nc.scalar.copy(
                out=bias_rows[:, first : first + experts_per_round, :],
                in_=bias_ps[:].rearrange("p e c l -> p e (c l)")[:, :, skipped:],
            )

        rows_ps_of = {}

        def rows_layer(e):
            if e >= EXPERTS:
                return
            wide = slice(VECTOR_CHUNK * P, COLS)
            z_ps = psum.tile([P, 1, row_chunks * P], F32, tag="out")
            for g in range(PASSES):
                nc.tensor.matmul_mx(
                    out=z_ps[:, 0, :],
                    lhsT=h_words[:, e, LAST, g, :].bitcast(FP8X4),
                    lhsT_scale=h_scales[:, e, LAST, g, :],
                    rhs=w_words[:, e * PASSES + g, wide].bitcast(FP8X4),
                    rhs_scale=w_scales[:, e * PASSES + g, wide],
                    start=(g == 0),
                    stop=(g == PASSES - 1),
                )
            rows_ps_of[e] = z_ps

        def add_bias(e):
            z_rows = work.tile([P, 1, VECTOR_COLS], F32)
            nc.vector.tensor_tensor(
                out=z_rows[:],
                in0=rows_ps_of[e][:, :, skipped:],
                in1=bias_rows[:, e : e + 1, :],
                op=ALU.add,
            )
            z_of[("rows", e)] = [z_rows[:]]
            y_of[("rows", e)] = [y_rows[:, e : e + 1, :]]

        def weigh(e, agents):
            for n in agents if 0 <= e < EXPERTS else []:
                weight = mix_rows[:, LAST, n * EXPERTS + e : n * EXPERTS + e + 1]
                if e == 0:
                    nc.vector.tensor_scalar_mul(
                        out=out_rows[:, n, :], in0=y_rows[:, e, :], scalar1=weight
                    )
                else:
                    nc.vector.scalar_tensor_tensor(
                        out=out_rows[:, n, :],
                        in0=y_rows[:, e, :],
                        scalar=weight,
                        in1=out_rows[:, n, :],
                        op0=ALU.mult,
                        op1=ALU.add,
                    )

        first_other = AGENTS - OTHER_AGENTS
        products = keep.tile([P, EXPERTS, OTHER_AGENTS, VECTOR_COLS], F32)
        halves = keep.tile([P, EXPERTS // 2, OTHER_AGENTS, VECTOR_COLS], F32)

        def multiply_others(experts):
            for e in experts:
                for n in range(first_other, AGENTS):
                    nc.scalar.activation(
                        out=products[:, e, n - first_other, :],
                        in_=y_rows[:, e, :],
                        func=ACT.Identity,
                        scale=mix_rows[:, LAST, n * EXPERTS + e : n * EXPERTS + e + 1],
                    )

        def add_others(level):
            if level == 0:
                nc.gpsimd.tensor_tensor(
                    out=halves[:], in0=products[:, 0:4, :, :], in1=products[:, 4:8, :, :], op=ALU.add
                )
            if level == 1:
                nc.gpsimd.tensor_tensor(
                    out=products[:, 0:2, :, :],
                    in0=halves[:, 0:2, :, :],
                    in1=halves[:, 2:4, :, :],
                    op=ALU.add,
                )
            if level == 2:
                nc.gpsimd.tensor_tensor(
                    out=out_rows[:, first_other:AGENTS, :],
                    in0=products[:, 0, :, :],
                    in1=products[:, 1, :, :],
                    op=ALU.add,
                )
                nc.sync.dma_start(
                    out=out[BATCH - P : BATCH, first_other:AGENTS, VECTOR_FIRST:COLS],
                    in_=out_rows[:, first_other:AGENTS, :],
                )

        out_flat = out.rearrange("b n l -> (b n) l")
        rounds_per_item = 2

        def tensor_columns(t):
            return sum(tensor_width(c, t) for c in range(CHUNKS))

        def blocks_per_round_of(t):
            return BANK // (P * len([c for c in range(CHUNKS) if tensor_width(c, t) > 0]))

        block_items = []
        for t in range(ROW_TILES - 1, -1, -1):
            blocks_per_item = rounds_per_item * blocks_per_round_of(t)
            block_items.extend([(t, j) for j in range(0, BLOCKS_PER_TILE, blocks_per_item)])

        def rounds_of(q):
            t, begin = block_items[q]
            count = blocks_per_round_of(t)
            start = t * BLOCKS_PER_TILE + begin
            return [start + v * count for v in range(rounds_per_item)], count

        def spread_blocks(q):
            t = block_items[q][0]
            firsts, count = rounds_of(q)
            chunks = [c for c in range(CHUNKS) if tensor_width(c, t) > 0]
            views = []
            for first in firsts:
                z_ps = psum.tile([P, count, len(chunks) * P], F32, tag="in")
                for j in range(first, first + count):
                    for c in chunks:
                        nc.tensor.transpose(
                            z_ps[:, j - first, c * P : (c + 1) * P],
                            zT_blocks[:, c, j, :, :].rearrange("p e i -> p (e i)"),
                            identity[:],
                        )
                views.append(z_ps[:, :, 0 : tensor_columns(t)])
            z_of[("blocks", q)] = views

        def place_blocks(q):
            t = block_items[q][0]
            count = rounds_of(q)[1]
            y_blocks = work.tile([P, rounds_per_item, count, tensor_columns(t)], F32)
            y_of[("blocks", q)] = [y_blocks[:, v, :, :] for v in range(rounds_per_item)]

        def combine_blocks(q):
            width = tensor_columns(block_items[q][0])
            firsts, blocks_per_round = rounds_of(q)
            for v in range(rounds_per_item):
                first = firsts[v]
                sum_ps = psum.tile([P, blocks_per_round, width], F32, tag="out")
                for j in range(first, first + blocks_per_round):
                    nc.tensor.matmul(
                        out=sum_ps[:, j - first, :],
                        lhsT=mix_blocks[:, j, :, :].rearrange("p i n -> p (i n)"),
                        rhs=y_of[("blocks", q)][v][:, j - first, :],
                        start=True,
                        stop=True,
                    )
                out_blocks = work.tile([P, blocks_per_round, width], F32)
                nc.scalar.copy(out=out_blocks[:], in_=sum_ps[:])
                queue = nc.scalar if q == len(block_items) - 1 else nc.sync
                queue.dma_start(
                    out=out_flat[
                        first * P : (first + blocks_per_round) * P, 0:width
                    ].rearrange("(j m) l -> m j l", m=P),
                    in_=out_blocks[:],
                )

        chain = [("blocks", q) for q in range(len(block_items))]

        def item_at(k):
            return chain[k] if 0 <= k < len(chain) else None

        def chain_step(k):
            ahead, new, mid, old, older = [item_at(k + 1 - d) for d in range(5)]
            if ahead is not None:
                spread_blocks(ahead[1])
            find_tops(new, range(len(z_of[new])))
            if old is not None and old[1] >= GPSIMD_SUMS:
                place_blocks(old[1])
                scale_powers(old, nc.gpsimd)
            raise_powers(new, [0])
            if mid is not None and mid[1] >= GPSIMD_SUMS:
                sum_powers(mid)
            raise_powers(new, range(1, len(z_of[new])))
            if mid is not None and mid[1] >= GPSIMD_SUMS:
                invert_sums(mid)
            if old is not None and old[1] < GPSIMD_SUMS:
                invert_sums(old)
                place_blocks(old[1])
                scale_powers(old, nc.gpsimd)
            if older is not None:
                combine_blocks(older[1])

        find_tops("mix rows", [0])
        mark_rows()
        raise_powers("mix rows")
        nc.vector.tensor_copy(out=b3_wide[:], in_=b3_rows[:])
        turn(0, LAST)
        group(0, LAST)
        sum_powers("mix rows")
        transpose_bias()
        invert_sums("mix rows")
        quantise(0, LAST)
        scale_powers("mix rows", nc.vector)
        turn(0, 0)
        group(0, 0)
        spread_mix(0)
        quantise(0, 0)
        rows_layer(0)
        spread_bias(0)
        turn(1, LAST)
        group(1, LAST)
        spread_bias(1)
        spread_mix(1)
        turn(1, 0)
        group(1, 0)
        spread_bias(2)
        spread_bias(3)

        def rows_item(e):
            return ("rows", e) if 0 <= e < EXPERTS else None

        early = [(e, n) for e in range(EXPERTS - 2) for n in range(first_other)]
        weighed = {"count": 0}

        def weigh_early(step, count):
            for e, n in early[weighed["count"] : weighed["count"] + count]:
                if e <= step - 2:
                    weigh(e, [n])
                    weighed["count"] = weighed["count"] + 1

        for e in range(EXPERTS + 1):
            new, mid = rows_item(e), rows_item(e - 1)
            turn(e + 2, LAST)
            turn(e + 2, 0)
            keep_blocks(e - 1)
            if new is not None:
                add_bias(e)
            quantise(e + 1, LAST)
            rows_layer(e + 1)
            blocks_layer(e)
            group(e + 2, LAST)
            if mid is not None:
                sum_powers(mid)
            weigh_early(e, 2)
            if new is not None:
                find_tops(new, [0])
            if mid is not None:
                invert_sums(mid)
            weigh_early(e, 2)
            if new is not None:
                raise_powers(new)
            group(e + 2, 0)
            if mid is not None:
                scale_powers(mid, nc.vector)
            weigh_early(e, STEP_WEIGHINGS - 4)
            quantise(e + 1, 0)
        spread_blocks(0)
        multiply_others(range(0, EXPERTS // 2))
        for k in range(len(chain)):
            chain_step(k)
            if k < GPSIMD_SUMS:
                sum_on_gpsimd(chain[k])
            if k == 0:
                multiply_others(range(EXPERTS // 2, EXPERTS))
                add_others(0)
            if k == 1:
                add_others(1)
                add_others(2)
            if k == 1:
                build_mix_blocks(LAST)
            if k == 2:
                build_mix_blocks(0)
        last = len(block_items) - 1
        kept = [(e, n) for e in range(EXPERTS - 2, EXPERTS) for n in range(first_other)]
        filled = {"count": 0}

        def fill(count):
            for e, n in kept[filled["count"] : filled["count"] + count]:
                weigh(e, [n])
                begin = n - n % STORE_AGENTS
                if e == EXPERTS - 1 and (n + 1 - begin == STORE_AGENTS or n + 1 == first_other):
                    nc.sync.dma_start(
                        out=out[BATCH - P : BATCH, begin : n + 1, VECTOR_FIRST:COLS],
                        in_=out_rows[:, begin : n + 1, :],
                    )
            filled["count"] = filled["count"] + count

        place_blocks(last - 1)
        scale_powers(("blocks", last - 1), nc.gpsimd)
        combine_blocks(last - 2)
        sum_powers(("blocks", last))
        invert_sums(("blocks", last))
        place_blocks(last)
        scale_powers(("blocks", last), nc.vector)
        combine_blocks(last - 1)
        fill(len(kept) - filled["count"])
        combine_blocks(last)
